import numpy as np
import ml_dtypes


BF16 = ml_dtypes.bfloat16


def bf(x):
    return np.asarray(x, np.float32).astype(BF16)


def f64(x):
    return np.asarray(x).astype(np.float64)


E2M1 = np.array([0.0, 0.5, 1.0, 1.5, 2.0, 3.0, 4.0, 6.0, -0.0, -0.5, -1.0, -1.5, -2.0, -3.0, -4.0, -6.0])


def pack_weight(w, fmt):
    k, n = w.shape
    w = f64(bf(w)).reshape(k // 32, 32, n)
    amax = np.abs(w).max(1)
    if fmt == "e4m3":
        byte = np.frexp(amax)[1] - 1 + 127 - 7
    else:
        mant, ex = np.frexp(amax / 6.0)
        byte = np.where(mant > 0.5, ex, ex - 1) + 127
    byte = np.clip(np.where(amax > 0, byte, 1), 1, 254)
    scaled = (w * np.exp2(127.0 - byte)[:, None, :]).reshape(k, n).astype(np.float32)
    by_word = np.ascontiguousarray(scaled.reshape(k // 512, 128, 4, n).transpose(0, 1, 3, 2))
    if fmt == "e4m3":
        words = by_word.astype(ml_dtypes.float8_e4m3fn).view(np.uint8)
    else:
        c = by_word.astype(ml_dtypes.float4_e2m1fn).view(np.uint8) & 0xF
        words = c[..., 0::2] | (c[..., 1::2] << 4)
    return np.ascontiguousarray(words), np.ascontiguousarray(byte.astype(np.uint8).reshape(k // 512, 16, n))


def unpack_weight(words, scales, fmt):
    g, p, n, _ = words.shape
    if fmt == "e4m3":
        vals = np.ascontiguousarray(words).view(ml_dtypes.float8_e4m3fn).astype(np.float64)
    else:
        nib = np.empty((g, p, n, 4), np.uint8)
        nib[..., 0::2] = words & 0xF
        nib[..., 1::2] = words >> 4
        vals = E2M1[nib]
    vals = vals * np.repeat(np.exp2(scales.astype(np.float64) - 127.0), 8, axis=1)[..., None]
    return vals.transpose(0, 1, 3, 2).reshape(g * 512, n)

def pack4(w):
    words, scales = pack_weight(w, "e2m1")
    return words.reshape(words.shape[0], 128, -1), scales


def unpack4(words, scales):
    return unpack_weight(words.reshape(words.shape[0], 128, -1, 2), scales, "e2m1")


def kspread(k):
    return np.exp2(np.repeat(np.random.randint(-6, 7, k // 32), 32).astype(np.float64))


B, T, C, H, KV, D = 2, 512, 8192, 16, 4, 128
EPS = 1e-5
THETA = 10000.0


def rmsnorm(h, w):
    var = np.mean(np.square(h), axis=-1, keepdims=True)
    return h * (1.0 / np.sqrt(var + EPS)) * w


def rope(h, cos, sin):
    hr = h.reshape(*h.shape[:-1], D // 2, 2)
    a, b = hr[..., 0], hr[..., 1]
    c = cos[None, :, None, :]
    s = sin[None, :, None, :]
    return np.stack([a * c - b * s, a * s + b * c], axis=-1).reshape(h.shape)


def setup_inputs():
    s = kspread(C)
    w_scale = 1.0 / np.sqrt(C)
    inv_freq = 1.0 / (THETA ** (np.arange(0, D, 2) / D))
    angles = np.arange(T)[:, None] * inv_freq[None, :]
    x = np.random.standard_normal((B, T, C)) * s
    x_words, x_scales = pack4(x.reshape(B * T, C).T)
    Wq_words, Wq_scales = pack4(np.random.standard_normal((C, H * D)) * w_scale / s[:, None])
    bq = bf(np.random.standard_normal(H * D) * 0.1)
    Wk_words, Wk_scales = pack4(np.random.standard_normal((C, KV * D)) * w_scale / s[:, None])
    bk = bf(np.random.standard_normal(KV * D) * 0.1)
    Wv_words, Wv_scales = pack4(np.random.standard_normal((C, KV * D)) * w_scale / s[:, None])
    bv = bf(np.random.standard_normal(KV * D) * 0.1)
    qn_w = bf(1.0 + 0.1 * np.random.standard_normal(D))
    kn_w = bf(1.0 + 0.1 * np.random.standard_normal(D))
    return {"x_words": x_words,
            "x_scales": x_scales,
            "Wq_words": Wq_words,
            "Wq_scales": Wq_scales,
            "bq": bq,
            "Wk_words": Wk_words,
            "Wk_scales": Wk_scales,
            "bk": bk,
            "Wv_words": Wv_words,
            "Wv_scales": Wv_scales,
            "bv": bv,
            "qn_w": qn_w,
            "kn_w": kn_w,
            "freqs_cos": bf(np.cos(angles)),
            "freqs_sin": bf(np.sin(angles))}


def reference(x_words, x_scales, Wq_words, Wq_scales, bq, Wk_words, Wk_scales, bk, Wv_words, Wv_scales, bv, qn_w, kn_w, freqs_cos, freqs_sin):
    xq = unpack4(x_words, x_scales).T.reshape(B, T, C)
    q = ((xq @ unpack4(Wq_words, Wq_scales)) + f64(bq)).reshape(B, T, H, D)
    k = ((xq @ unpack4(Wk_words, Wk_scales)) + f64(bk)).reshape(B, T, KV, D)
    v = ((xq @ unpack4(Wv_words, Wv_scales)) + f64(bv)).reshape(B, T, KV, D)
    q = rmsnorm(q, f64(qn_w))
    k = rmsnorm(k, f64(kn_w))
    q = rope(q, f64(freqs_cos), f64(freqs_sin))
    k = rope(k, f64(freqs_cos), f64(freqs_sin))
    return q, k, v

@@ -1,0 +1,267 @@
+from contextlib import ExitStack
+
+import concourse.mybir as mybir
+
+F32 = mybir.dt.float32
+BF16 = mybir.dt.bfloat16
+I32 = mybir.dt.int32
+U8 = mybir.dt.uint8
+FP4X4 = mybir.dt.float4_e2m1fn_x4
+ALU = mybir.AluOpType
+ACT = mybir.ActivationFunctionType
+
+P = 128
+PASSES = 16
+M_TILES = 8
+POS_TILES = 4
+N_TILE = 512
+HEAD = 128
+HEADS_PER_TILE = N_TILE // HEAD
+EPS = 1e-5
+FLOPS = 2 * 1024 * 8192 * 3072
+
+STREAM_RUNS = ((0, 1), (1, 4), (4, 8), (8, 12), (12, 16))
+CHUNK_RUNS = ((0, 4), (4, 8), (8, 12), (12, 16))
+
+
+def tile_llamacausalselfattention_pa_kernel(
+    tc,
+    x_words,
+    x_scales,
+    Wq_words,
+    Wq_scales,
+    bq,
+    Wk_words,
+    Wk_scales,
+    bk,
+    Wv_words,
+    Wv_scales,
+    bv,
+    qn_w,
+    kn_w,
+    freqs_cos,
+    freqs_sin,
+    out_0,
+    out_1,
+    out_2,
+):
+    nc = tc.nc
+    q_out = out_0.rearrange("b t h d -> (b t) (h d)")
+    k_out = out_1.rearrange("b t h d -> (b t) (h d)")
+    v_out = out_2.rearrange("b t h d -> (b t) (h d)")
+    col_tiles = [(Wq_words, Wq_scales, bq, N_TILE * c, q_out) for c in range(4)]
+    col_tiles.append((Wk_words, Wk_scales, bk, 0, k_out))
+    col_tiles.append((Wv_words, Wv_scales, bv, 0, v_out))
+
+    with ExitStack() as ctx:
+        ctx.enter_context(tc.manual_schedule())
+        keep = ctx.enter_context(tc.tile_pool(name="keep", bufs=1))
+        work = ctx.enter_context(tc.tile_pool(name="work", bufs=2))
+        psum = ctx.enter_context(tc.psum_pool(name="psum", bufs=8))
+
+        def load_codes(tag, words, g0, g1, byte0, nbytes):
+            codes = keep.tile([P, g1 - g0, nbytes], U8, name=tag, tag=tag, align_bytes=64)
+            nc.sync.dma_start(
+                out=codes[:].bitcast(I32),
+                in_=words[g0:g1, :, byte0 : byte0 + nbytes].rearrange("g p b -> p g b").bitcast(I32),
+            )
+            return codes
+
+        def load_planes(tag, scales, g0, g1, col0, ncols):
+            planes = keep.tile([P, g1 - g0, ncols], U8, name=tag, tag=tag, align_bytes=64)
+            nc.vector.memset(planes[:].bitcast(I32), 0)
+            for quad in range(4):
+                nc.sync.dma_start(
+                    out=planes[32 * quad : 32 * quad + 4, :, :].bitcast(I32),
+                    in_=scales[g0:g1, 4 * quad : 4 * quad + 4, col0 : col0 + ncols]
+                    .rearrange("g r n -> r g n")
+                    .bitcast(I32),
+                )
+            return planes
+
+        def load_col_tile(c, prefix, runs, per_pass_codes):
+            words, scales, col0 = col_tiles[c][0], col_tiles[c][1], col_tiles[c][3]
+            w_codes = {}
+            w_planes = {}
+            for g0, g1 in runs:
+                planes = load_planes("%sp%d" % (prefix, g0), scales, g0, g1, col0, N_TILE)
+                for g in range(g0, g1):
+                    w_planes[g] = planes[:, g - g0, :]
+                if per_pass_codes:
+                    for g in range(g0, g1):
+                        codes = load_codes("%sc%d" % (prefix, g), words, g, g + 1, 2 * col0, 2 * N_TILE)
+                        w_codes[g] = codes[:, 0, :]
+                else:
+                    codes = load_codes("%sc%d" % (prefix, g0), words, g0, g1, 2 * col0, 2 * N_TILE)
+                    for g in range(g0, g1):
+                        w_codes[g] = codes[:, g - g0, :]
+            return w_codes, w_planes
+
+        x_codes = {}
+        x_planes = {}
+        w_codes = {}
+        w_planes = {}
+        w_codes[0] = {}
+        w_planes[0] = {}
+        for g0, g1 in STREAM_RUNS:
+            xp = load_planes("xp%d" % g0, x_scales, g0, g1, 0, 1024)
+            wp = load_planes("sp%d" % g0, Wq_scales, g0, g1, 0, N_TILE)
+            for g in range(g0, g1):
+                x_planes[g] = xp[:, g - g0, :]
+                w_planes[0][g] = wp[:, g - g0, :]
+                xc = load_codes("xc%d" % g, x_words, g, g + 1, 0, 2048)
+                x_codes[g] = xc[:, 0, :]
+                wc = load_codes("sc%d" % g, Wq_words, g, g + 1, 0, 2 * N_TILE)
+                w_codes[0][g] = wc[:, 0, :]
+
+        eps_t = keep.tile([P, 1], F32, name="eps_t")
+        nc.vector.memset(eps_t[:], EPS)
+        warm = keep.tile([P, 1], F32, name="warm")
+        nc.scalar.activation(out=warm[:], in_=eps_t[:], func=ACT.Sqrt)
+
+        cos_raw = keep.tile([P, POS_TILES, HEAD // 2], BF16, name="cos_raw")
+        sin_raw = keep.tile([P, POS_TILES, HEAD // 2], BF16, name="sin_raw")
+        nc.sync.dma_start(out=cos_raw[:], in_=freqs_cos.rearrange("(t p) j -> p t j", p=P))
+        nc.sync.dma_start(out=sin_raw[:], in_=freqs_sin.rearrange("(t p) j -> p t j", p=P))
+        gains = {}
+        for nm, w in (("q", qn_w), ("k", kn_w)):
+            g_b = keep.tile([P, HEAD], BF16, name="gain_" + nm)
+            nc.sync.dma_start(out=g_b[:], in_=w.partition_broadcast(P))
+            gains[nm] = g_b
+        bias = {}
+
+        def load_bias(c):
+            b_t = keep.tile([P, N_TILE], BF16, name="bias%d" % c)
+            b_src, col0 = col_tiles[c][2], col_tiles[c][3]
+            nc.sync.dma_start(out=b_t[:], in_=b_src[col0 : col0 + N_TILE].partition_broadcast(P))
+            bias[c] = b_t
+
+        load_bias(0)
+        w_codes[1], w_planes[1] = load_col_tile(1, "w1", CHUNK_RUNS, False)
+        for c in range(1, 6):
+            load_bias(c)
+        for c in (2, 3, 4):
+            w_codes[c], w_planes[c] = load_col_tile(c, "w%d" % c, ((0, 16),), False)
+
+        tabs = {}
+        for nm in ("q", "k"):
+            g3 = gains[nm][:].rearrange("p (j e) -> p j e", e=2)
+            gsw = keep.tile([P, HEAD // 2, 2], F32, name="gsw_" + nm)
+            nc.vector.tensor_scalar(
+                out=gsw[:, :, 0:1], in0=g3[:, :, 1:2], scalar1=-1.0, scalar2=None, op0=ALU.mult
+            )
+            nc.vector.tensor_copy(out=gsw[:, :, 1:2], in_=g3[:, :, 0:1])
+            tab_c = keep.tile([P, POS_TILES, HEAD], F32, name="tabc_" + nm)
+            tab_s = keep.tile([P, POS_TILES, HEAD], F32, name="tabs_" + nm)
+            for t in range(POS_TILES):
+                nc.vector.tensor_tensor(
+                    out=tab_c[:, t, :].rearrange("p (j e) -> p j e", e=2),
+                    in0=g3,
+                    in1=cos_raw[:, t, :].unsqueeze(2).to_broadcast([P, HEAD // 2, 2]),
+                    op=ALU.mult,
+                )
+                nc.vector.tensor_tensor(
+                    out=tab_s[:, t, :].rearrange("p (j e) -> p j e", e=2),
+                    in0=gsw[:],
+                    in1=sin_raw[:, t, :].unsqueeze(2).to_broadcast([P, HEAD // 2, 2]),
+                    op=ALU.mult,
+                )
+            tabs[nm] = (tab_c, tab_s)
+
+        def new_acc():
+            acc = psum.tile([P, N_TILE], F32, name="acc", tag="acc")
+            return acc
+
+        def mm(acc, c, m, g):
+            nc.tensor.matmul_mx(
+                out=acc[:],
+                lhsT=x_codes[g][:, 256 * m : 256 * (m + 1)].bitcast(FP4X4),
+                lhsT_scale=x_planes[g][:, P * m : P * (m + 1)],
+                rhs=w_codes[c][g].bitcast(FP4X4),
+                rhs_scale=w_planes[c][g],
+                start=(g == 0),
+                stop=(g == PASSES - 1),
+            )
+
+        def out_slice(c, m):
+            col0, dst = col_tiles[c][3], col_tiles[c][4]
+            return dst[P * m : P * (m + 1), col0 : col0 + N_TILE]
+
+        def stage_a(acc, c, m):
+            if c == 5:
+                res = work.tile([P, N_TILE], F32, name="res", tag="res", bufs=3)
+                nc.vector.tensor_tensor(out=res[:], in0=acc[:], in1=bias[c][:], op=ALU.add)
+                nc.sync.dma_start(out=out_slice(c, m), in_=res[:])
+                return None
+            h = work.tile([P, N_TILE], F32, name="h", tag="h", bufs=8)
+            nc.vector.tensor_tensor(out=h[:], in0=acc[:], in1=bias[c][:], op=ALU.add)
+            ss = work.tile([P, HEADS_PER_TILE], F32, name="ss", tag="ss", bufs=9)
+            rms = work.tile([P, HEADS_PER_TILE], F32, name="rms", tag="rms", bufs=9)
+            for n in range(HEADS_PER_TILE):
+                junk = work.tile([P, HEAD], F32, name="junk", tag="junk", bufs=2)
+                nc.scalar.activation(
+                    out=junk[:],
+                    in_=h[:, HEAD * n : HEAD * (n + 1)],
+                    func=ACT.Square,
+                    accum_out=ss[:, n : n + 1],
+                )
+            nc.scalar.activation(out=rms[:], in_=ss[:], func=ACT.Sqrt, bias=eps_t[:], scale=1.0 / HEAD)
+            return h, rms
+
+        def stage_b(state, c, m):
+            if state is None:
+                return
+            h, rms = state
+            tab_c, tab_s = tabs["q" if c < 4 else "k"]
+            t = m % POS_TILES
+            t1 = work.tile([P, N_TILE], F32, name="t1", tag="t1", bufs=3)
+            t2 = work.tile([P, N_TILE], F32, name="t2", tag="t2", bufs=2)
+            nc.vector.tensor_tensor(
+                out=t1[:].rearrange("p (n d) -> p n d", d=HEAD),
+                in0=h[:].rearrange("p (n d) -> p n d", d=HEAD),
+                in1=tab_c[:, t, :].unsqueeze(1).to_broadcast([P, HEADS_PER_TILE, HEAD]),
+                op=ALU.mult,
+            )
+            nc.vector.tensor_tensor(
+                out=t2[:].rearrange("p (n j e) -> p n j e", n=HEADS_PER_TILE, e=2),
+                in0=h[:].rearrange("p (n j e) -> p n j e", n=HEADS_PER_TILE, e=2)[:, :, :, ::-1],
+                in1=tab_s[:, t, :]
+                .rearrange("p (j e) -> p j e", e=2)
+                .unsqueeze(1)
+                .to_broadcast([P, HEADS_PER_TILE, HEAD // 2, 2]),
+                op=ALU.mult,
+            )
+            nc.vector.tensor_tensor(out=t1[:], in0=t1[:], in1=t2[:], op=ALU.add)
+            rstd = work.tile([P, HEADS_PER_TILE], F32, name="rstd", tag="rstd", bufs=3)
+            nc.vector.reciprocal(out=rstd[:], in_=rms[:])
+            res = work.tile([P, N_TILE], F32, name="res", tag="res", bufs=3)
+            for n in range(HEADS_PER_TILE):
+                nc.scalar.activation(
+                    out=res[:, HEAD * n : HEAD * (n + 1)],
+                    in_=t1[:, HEAD * n : HEAD * (n + 1)],
+                    func=ACT.Copy,
+                    scale=rstd[:, n : n + 1],
+                )
+            nc.scalar.dma_start(out=out_slice(c, m), in_=res[:])
+
+        def sweep(c, ms):
+            accs = [new_acc() for m in ms]
+            for g in range(PASSES):
+                for acc, m in zip(accs, ms):
+                    mm(acc, c, m, g)
+            states = [stage_a(acc, c, m) for acc, m in zip(accs, ms)]
+            return states
+
+        ms_all = list(range(M_TILES))
+        states = sweep(0, ms_all)
+        for st, m in zip(states, ms_all):
+            stage_b(st, 0, m)
+        for ms in (ms_all[:4], ms_all[4:]):
+            states = sweep(1, ms)
+            for st, m in zip(states, ms):
+                stage_b(st, 1, m)
+        w_codes[5], w_planes[5] = load_col_tile(5, "s", STREAM_RUNS, True)
+        for c in (2, 3, 4, 5):
+            for m in ms_all:
+                states = sweep(c, [m])
+                stage_b(states[0], c, m)

@@ -21,6 +21,7 @@ EPS = 1e-5
 FLOPS = 2 * 1024 * 8192 * 3072
 
 STREAM_RUNS = ((0, 1), (1, 4), (4, 8), (8, 12), (12, 16))
+N_WARM = 9
 CHUNK_RUNS = ((0, 4), (4, 8), (8, 12), (12, 16))
 
 
@@ -97,13 +98,40 @@ def tile_llamacausalselfattention_pa_kernel(
                         w_codes[g] = codes[:, g - g0, :]
             return w_codes, w_planes
 
+        warm_sb = keep.tile([P, N_TILE], BF16, name="warm_sb")
+        nc.gpsimd.memset(warm_sb[:], 0.0)
+        warm_acc = psum.tile([P, N_TILE], F32, name="acc", tag="acc")
+        for i in range(N_WARM):
+            nc.tensor.matmul(out=warm_acc[:], lhsT=warm_sb[:, 0:P], rhs=warm_sb[:], start=True, stop=True)
+
         x_codes = {}
         x_planes = {}
         w_codes = {}
         w_planes = {}
         w_codes[0] = {}
         w_planes[0] = {}
-        for g0, g1 in STREAM_RUNS:
+        xp = keep.tile([P, 1, 1024], U8, name="xp0", tag="xp0", align_bytes=64)
+        wp = keep.tile([P, 1, N_TILE], U8, name="sp0", tag="sp0", align_bytes=64)
+
+        def fill_quad(planes, scales, quad, ncols):
+            nc.sync.dma_start(
+                out=planes[32 * quad : 32 * quad + 32, 0, :].bitcast(I32),
+                in_=scales.rearrange("g r n -> (g r) n")[4 * quad : 4 * quad + 32, 0:ncols].bitcast(I32),
+            )
+
+        fill_quad(xp, x_scales, 0, 1024)
+        fill_quad(xp, x_scales, 1, 1024)
+        xc = load_codes("xc0", x_words, 0, 1, 0, 2048)
+        wc = load_codes("sc0", Wq_words, 0, 1, 0, 2 * N_TILE)
+        fill_quad(xp, x_scales, 2, 1024)
+        fill_quad(xp, x_scales, 3, 1024)
+        for quad in range(4):
+            fill_quad(wp, Wq_scales, quad, N_TILE)
+        x_planes[0] = xp[:, 0, :]
+        w_planes[0][0] = wp[:, 0, :]
+        x_codes[0] = xc[:, 0, :]
+        w_codes[0][0] = wc[:, 0, :]
+        for g0, g1 in STREAM_RUNS[1:]:
             xp = load_planes("xp%d" % g0, x_scales, g0, g1, 0, 1024)
             wp = load_planes("sp%d" % g0, Wq_scales, g0, g1, 0, N_TILE)
             for g in range(g0, g1):
@@ -168,30 +196,30 @@ def tile_llamacausalselfattention_pa_kernel(
                 )
             tabs[nm] = (tab_c, tab_s)
 
-        def new_acc():
-            acc = psum.tile([P, N_TILE], F32, name="acc", tag="acc")
+        def new_acc(n):
+            acc = psum.tile([P, n], F32, name="acc", tag="acc")
             return acc
 
-        def mm(acc, c, m, g):
+        def mm(acc, c, m, g, n0=0, n=N_TILE):
             nc.tensor.matmul_mx(
                 out=acc[:],
                 lhsT=x_codes[g][:, 256 * m : 256 * (m + 1)].bitcast(FP4X4),
                 lhsT_scale=x_planes[g][:, P * m : P * (m + 1)],
-                rhs=w_codes[c][g].bitcast(FP4X4),
-                rhs_scale=w_planes[c][g],
+                rhs=w_codes[c][g][:, 2 * n0 : 2 * (n0 + n)].bitcast(FP4X4),
+                rhs_scale=w_planes[c][g][:, n0 : n0 + n],
                 start=(g == 0),
                 stop=(g == PASSES - 1),
             )
 
-        def out_slice(c, m):
+        def out_slice(c, m, n0=0, n=N_TILE):
             col0, dst = col_tiles[c][3], col_tiles[c][4]
-            return dst[P * m : P * (m + 1), col0 : col0 + N_TILE]
+            return dst[P * m : P * (m + 1), col0 + n0 : col0 + n0 + n]
 
-        def stage_a(acc, c, m):
+        def stage_a(acc, c, m, n0=0, n=N_TILE):
             if c == 5:
-                res = work.tile([P, N_TILE], F32, name="res", tag="res", bufs=3)
-                nc.vector.tensor_tensor(out=res[:], in0=acc[:], in1=bias[c][:], op=ALU.add)
-                nc.sync.dma_start(out=out_slice(c, m), in_=res[:])
+                res = work.tile([P, n], F32, name="res", tag="res", bufs=3)
+                nc.vector.tensor_tensor(out=res[:], in0=acc[:], in1=bias[c][:, n0 : n0 + n], op=ALU.add)
+                nc.sync.dma_start(out=out_slice(c, m, n0, n), in_=res[:])
                 return None
             h = work.tile([P, N_TILE], F32, name="h", tag="h", bufs=8)
             nc.vector.tensor_tensor(out=h[:], in0=acc[:], in1=bias[c][:], op=ALU.add)
@@ -245,7 +273,7 @@ def tile_llamacausalselfattention_pa_kernel(
             nc.scalar.dma_start(out=out_slice(c, m), in_=res[:])
 
         def sweep(c, ms):
-            accs = [new_acc() for m in ms]
+            accs = [new_acc(N_TILE) for m in ms]
             for g in range(PASSES):
                 for acc, m in zip(accs, ms):
                     mm(acc, c, m, g)
@@ -263,5 +291,12 @@ def tile_llamacausalselfattention_pa_kernel(
         w_codes[5], w_planes[5] = load_col_tile(5, "s", STREAM_RUNS, True)
         for c in (2, 3, 4, 5):
             for m in ms_all:
+                if c == 5 and m == M_TILES - 1:
+                    break
                 states = sweep(c, [m])
                 stage_b(states[0], c, m)
+        for n0 in (0, N_TILE // 2):
+            acc = new_acc(N_TILE // 2)
+            for g in range(PASSES):
+                mm(acc, 5, M_TILES - 1, g, n0, N_TILE // 2)
+            stage_a(acc, 5, M_TILES - 1, n0, N_TILE // 2)

@@ -110,37 +110,44 @@ def tile_llamacausalselfattention_pa_kernel(
         w_planes = {}
         w_codes[0] = {}
         w_planes[0] = {}
-        xp = keep.tile([P, 1, 1024], U8, name="xp0", tag="xp0", align_bytes=64)
-        wp = keep.tile([P, 1, N_TILE], U8, name="sp0", tag="sp0", align_bytes=64)
-
         def fill_quad(planes, scales, quad, ncols):
             nc.sync.dma_start(
                 out=planes[32 * quad : 32 * quad + 32, 0, :].bitcast(I32),
                 in_=scales.rearrange("g r n -> (g r) n")[4 * quad : 4 * quad + 32, 0:ncols].bitcast(I32),
             )
 
-        fill_quad(xp, x_scales, 0, 1024)
-        fill_quad(xp, x_scales, 1, 1024)
-        xc = load_codes("xc0", x_words, 0, 1, 0, 2048)
-        wc = load_codes("sc0", Wq_words, 0, 1, 0, 2 * N_TILE)
-        fill_quad(xp, x_scales, 2, 1024)
-        fill_quad(xp, x_scales, 3, 1024)
-        for quad in range(4):
-            fill_quad(wp, Wq_scales, quad, N_TILE)
-        x_planes[0] = xp[:, 0, :]
-        w_planes[0][0] = wp[:, 0, :]
-        x_codes[0] = xc[:, 0, :]
-        w_codes[0][0] = wc[:, 0, :]
-        for g0, g1 in STREAM_RUNS[1:]:
+        def x_plane_run(g0, g1):
             xp = load_planes("xp%d" % g0, x_scales, g0, g1, 0, 1024)
-            wp = load_planes("sp%d" % g0, Wq_scales, g0, g1, 0, N_TILE)
             for g in range(g0, g1):
                 x_planes[g] = xp[:, g - g0, :]
+
+        def w_plane_run(g0, g1):
+            wp = load_planes("sp%d" % g0, Wq_scales, g0, g1, 0, N_TILE)
+            for g in range(g0, g1):
                 w_planes[0][g] = wp[:, g - g0, :]
-                xc = load_codes("xc%d" % g, x_words, g, g + 1, 0, 2048)
-                x_codes[g] = xc[:, 0, :]
-                wc = load_codes("sc%d" % g, Wq_words, g, g + 1, 0, 2 * N_TILE)
-                w_codes[0][g] = wc[:, 0, :]
+
+        def code_pass(g):
+            xc = load_codes("xc%d" % g, x_words, g, g + 1, 0, 2048)
+            x_codes[g] = xc[:, 0, :]
+            wc = load_codes("sc%d" % g, Wq_words, g, g + 1, 0, 2 * N_TILE)
+            w_codes[0][g] = wc[:, 0, :]
+
+        wp0 = keep.tile([P, 1, N_TILE], U8, name="sp0", tag="sp0", align_bytes=64)
+        w_planes[0][0] = wp0[:, 0, :]
+        fill_quad(wp0, Wq_scales, 0, N_TILE)
+        fill_quad(wp0, Wq_scales, 1, N_TILE)
+        x_plane_run(0, 4)
+        code_pass(0)
+        fill_quad(wp0, Wq_scales, 2, N_TILE)
+        fill_quad(wp0, Wq_scales, 3, N_TILE)
+        w_plane_run(1, 4)
+        for g in range(1, 4):
+            code_pass(g)
+        for g0, g1 in CHUNK_RUNS[1:]:
+            x_plane_run(g0, g1)
+            w_plane_run(g0, g1)
+            for g in range(g0, g1):
+                code_pass(g)
 
         eps_t = keep.tile([P, 1], F32, name="eps_t")
         nc.vector.memset(eps_t[:], EPS)

@@ -11,18 +11,26 @@ ALU = mybir.AluOpType
 ACT = mybir.ActivationFunctionType
 
 P = 128
+K_PASS = 512
 PASSES = 16
-M_TILES = 8
-POS_TILES = 4
-N_TILE = 512
+TOKENS = 1024
+TOKEN_TILES = TOKENS // P
+POSITION_TILES = 4
+COLS = 512
 HEAD = 128
-HEADS_PER_TILE = N_TILE // HEAD
+HEADS = COLS // HEAD
+PAIRS = HEAD // 2
+QUADRANTS = 4
+K_TILE = 4
+V_TILE = 5
 EPS = 1e-5
-FLOPS = 2 * 1024 * 8192 * 3072
+FLOPS = 2 * TOKENS * (PASSES * K_PASS) * ((V_TILE + 1) * COLS)
 
-STREAM_RUNS = ((0, 1), (1, 4), (4, 8), (8, 12), (12, 16))
-N_WARM = 9
-CHUNK_RUNS = ((0, 4), (4, 8), (8, 12), (12, 16))
+FIRST_SWEEP_RUNS = ((0, 1), (1, 4), (4, 8), (8, 12), (12, 16))
+SECOND_SWEEP_RUNS = ((0, 4), (4, 8), (8, 12), (12, 16))
+WHOLE_RUN = ((0, PASSES),)
+
+WARM_MATMULS = 9
 
 
 def tile_llamacausalselfattention_pa_kernel(
@@ -50,15 +58,22 @@ def tile_llamacausalselfattention_pa_kernel(
     q_out = out_0.rearrange("b t h d -> (b t) (h d)")
     k_out = out_1.rearrange("b t h d -> (b t) (h d)")
     v_out = out_2.rearrange("b t h d -> (b t) (h d)")
-    col_tiles = [(Wq_words, Wq_scales, bq, N_TILE * c, q_out) for c in range(4)]
-    col_tiles.append((Wk_words, Wk_scales, bk, 0, k_out))
-    col_tiles.append((Wv_words, Wv_scales, bv, 0, v_out))
+    sources = [(Wq_words, Wq_scales, bq, COLS * c, q_out) for c in range(K_TILE)]
+    sources.append((Wk_words, Wk_scales, bk, 0, k_out))
+    sources.append((Wv_words, Wv_scales, bv, 0, v_out))
 
     with ExitStack() as ctx:
         ctx.enter_context(tc.manual_schedule())
         keep = ctx.enter_context(tc.tile_pool(name="keep", bufs=1))
         work = ctx.enter_context(tc.tile_pool(name="work", bufs=2))
         psum = ctx.enter_context(tc.psum_pool(name="psum", bufs=8))
+
+        zeros = keep.tile([P, COLS], BF16, name="zeros")
+        nc.gpsimd.memset(zeros[:], 0.0)
+        dummy_bank = psum.tile([P, COLS], F32, name="bank", tag="bank")
+        for i in range(WARM_MATMULS):
+            nc.tensor.matmul(out=dummy_bank[:], lhsT=zeros[:, 0:P], rhs=zeros[:], start=True, stop=True)
+
 
         def load_codes(tag, words, g0, g1, byte0, nbytes):
             codes = keep.tile([P, g1 - g0, nbytes], U8, name=tag, tag=tag, align_bytes=64)
@@ -71,7 +86,7 @@ def tile_llamacausalselfattention_pa_kernel(
         def load_planes(tag, scales, g0, g1, col0, ncols):
             planes = keep.tile([P, g1 - g0, ncols], U8, name=tag, tag=tag, align_bytes=64)
             nc.vector.memset(planes[:].bitcast(I32), 0)
-            for quad in range(4):
+            for quad in range(QUADRANTS):
                 nc.sync.dma_start(
                     out=planes[32 * quad : 32 * quad + 4, :, :].bitcast(I32),
                     in_=scales[g0:g1, 4 * quad : 4 * quad + 4, col0 : col0 + ncols]
@@ -80,230 +95,202 @@ def tile_llamacausalselfattention_pa_kernel(
                 )
             return planes
 
-        def load_col_tile(c, prefix, runs, per_pass_codes):
-            words, scales, col0 = col_tiles[c][0], col_tiles[c][1], col_tiles[c][3]
-            w_codes = {}
-            w_planes = {}
-            for g0, g1 in runs:
-                planes = load_planes("%sp%d" % (prefix, g0), scales, g0, g1, col0, N_TILE)
-                for g in range(g0, g1):
-                    w_planes[g] = planes[:, g - g0, :]
-                if per_pass_codes:
-                    for g in range(g0, g1):
-                        codes = load_codes("%sc%d" % (prefix, g), words, g, g + 1, 2 * col0, 2 * N_TILE)
-                        w_codes[g] = codes[:, 0, :]
-                else:
-                    codes = load_codes("%sc%d" % (prefix, g0), words, g0, g1, 2 * col0, 2 * N_TILE)
-                    for g in range(g0, g1):
-                        w_codes[g] = codes[:, g - g0, :]
-            return w_codes, w_planes
-
-        warm_sb = keep.tile([P, N_TILE], BF16, name="warm_sb")
-        nc.gpsimd.memset(warm_sb[:], 0.0)
-        warm_acc = psum.tile([P, N_TILE], F32, name="acc", tag="acc")
-        for i in range(N_WARM):
-            nc.tensor.matmul(out=warm_acc[:], lhsT=warm_sb[:, 0:P], rhs=warm_sb[:], start=True, stop=True)
-
-        x_codes = {}
-        x_planes = {}
-        w_codes = {}
-        w_planes = {}
-        w_codes[0] = {}
-        w_planes[0] = {}
-        def fill_quad(planes, scales, quad, ncols):
+        def fill_quadrant(planes, scales, quad, ncols):
             nc.sync.dma_start(
                 out=planes[32 * quad : 32 * quad + 32, 0, :].bitcast(I32),
                 in_=scales.rearrange("g r n -> (g r) n")[4 * quad : 4 * quad + 32, 0:ncols].bitcast(I32),
             )
 
-        def x_plane_run(g0, g1):
-            xp = load_planes("xp%d" % g0, x_scales, g0, g1, 0, 1024)
+        def load_column_tile(c, tag, plane_runs, codes_by_pass):
+            words, scales, col0 = sources[c][0], sources[c][1], sources[c][3]
+            codes_of = {}
+            plane_of = {}
+            for g0, g1 in plane_runs:
+                planes = load_planes("%sp%d" % (tag, g0), scales, g0, g1, col0, COLS)
+                for g in range(g0, g1):
+                    plane_of[g] = planes[:, g - g0, :]
+                if codes_by_pass:
+                    for g in range(g0, g1):
+                        codes = load_codes("%sc%d" % (tag, g), words, g, g + 1, 2 * col0, 2 * COLS)
+                        codes_of[g] = codes[:, 0, :]
+                else:
+                    codes = load_codes("%sc%d" % (tag, g0), words, g0, g1, 2 * col0, 2 * COLS)
+                    for g in range(g0, g1):
+                        codes_of[g] = codes[:, g - g0, :]
+            return codes_of, plane_of
+
+        x_codes_of = {}
+        x_plane_of = {}
+        w_codes_of = {0: {}}
+        w_plane_of = {0: {}}
+
+        x_run_planes = keep.tile([P, 1, TOKENS], U8, name="xp0", tag="xp0", align_bytes=64)
+        w_run_planes = keep.tile([P, 1, COLS], U8, name="w0p0", tag="w0p0", align_bytes=64)
+        fill_quadrant(x_run_planes, x_scales, 0, TOKENS)
+        fill_quadrant(x_run_planes, x_scales, 1, TOKENS)
+        x_codes_of[0] = load_codes("xc0", x_words, 0, 1, 0, 2 * TOKENS)[:, 0, :]
+        w_codes_of[0][0] = load_codes("w0c0", Wq_words, 0, 1, 0, 2 * COLS)[:, 0, :]
+        fill_quadrant(x_run_planes, x_scales, 2, TOKENS)
+        fill_quadrant(x_run_planes, x_scales, 3, TOKENS)
+        for quad in range(QUADRANTS):
+            fill_quadrant(w_run_planes, Wq_scales, quad, COLS)
+        x_plane_of[0] = x_run_planes[:, 0, :]
+        w_plane_of[0][0] = w_run_planes[:, 0, :]
+
+        for g0, g1 in FIRST_SWEEP_RUNS[1:]:
+            x_run_planes = load_planes("xp%d" % g0, x_scales, g0, g1, 0, TOKENS)
+            w_run_planes = load_planes("w0p%d" % g0, Wq_scales, g0, g1, 0, COLS)
             for g in range(g0, g1):
-                x_planes[g] = xp[:, g - g0, :]
+                x_plane_of[g] = x_run_planes[:, g - g0, :]
+                w_plane_of[0][g] = w_run_planes[:, g - g0, :]
+                x_codes_of[g] = load_codes("xc%d" % g, x_words, g, g + 1, 0, 2 * TOKENS)[:, 0, :]
+                w_codes_of[0][g] = load_codes("w0c%d" % g, Wq_words, g, g + 1, 0, 2 * COLS)[:, 0, :]
 
-        def w_plane_run(g0, g1):
-            wp = load_planes("sp%d" % g0, Wq_scales, g0, g1, 0, N_TILE)
-            for g in range(g0, g1):
-                w_planes[0][g] = wp[:, g - g0, :]
+        eps = keep.tile([P, 1], F32, name="eps")
+        nc.vector.memset(eps[:], EPS)
+        table_warmer = keep.tile([P, 1], F32, name="table_warmer")
+        nc.scalar.activation(out=table_warmer[:], in_=eps[:], func=ACT.Sqrt)
 
-        def code_pass(g):
-            xc = load_codes("xc%d" % g, x_words, g, g + 1, 0, 2048)
-            x_codes[g] = xc[:, 0, :]
-            wc = load_codes("sc%d" % g, Wq_words, g, g + 1, 0, 2 * N_TILE)
-            w_codes[0][g] = wc[:, 0, :]
-
-        wp0 = keep.tile([P, 1, N_TILE], U8, name="sp0", tag="sp0", align_bytes=64)
-        w_planes[0][0] = wp0[:, 0, :]
-        fill_quad(wp0, Wq_scales, 0, N_TILE)
-        fill_quad(wp0, Wq_scales, 1, N_TILE)
-        x_plane_run(0, 4)
-        code_pass(0)
-        fill_quad(wp0, Wq_scales, 2, N_TILE)
-        fill_quad(wp0, Wq_scales, 3, N_TILE)
-        w_plane_run(1, 4)
-        for g in range(1, 4):
-            code_pass(g)
-        for g0, g1 in CHUNK_RUNS[1:]:
-            x_plane_run(g0, g1)
-            w_plane_run(g0, g1)
-            for g in range(g0, g1):
-                code_pass(g)
-
-        eps_t = keep.tile([P, 1], F32, name="eps_t")
-        nc.vector.memset(eps_t[:], EPS)
-        warm = keep.tile([P, 1], F32, name="warm")
-        nc.scalar.activation(out=warm[:], in_=eps_t[:], func=ACT.Sqrt)
-
-        cos_raw = keep.tile([P, POS_TILES, HEAD // 2], BF16, name="cos_raw")
-        sin_raw = keep.tile([P, POS_TILES, HEAD // 2], BF16, name="sin_raw")
-        nc.sync.dma_start(out=cos_raw[:], in_=freqs_cos.rearrange("(t p) j -> p t j", p=P))
-        nc.sync.dma_start(out=sin_raw[:], in_=freqs_sin.rearrange("(t p) j -> p t j", p=P))
-        gains = {}
-        for nm, w in (("q", qn_w), ("k", kn_w)):
-            g_b = keep.tile([P, HEAD], BF16, name="gain_" + nm)
-            nc.sync.dma_start(out=g_b[:], in_=w.partition_broadcast(P))
-            gains[nm] = g_b
+        cos = keep.tile([P, POSITION_TILES, PAIRS], BF16, name="cos")
+        sin = keep.tile([P, POSITION_TILES, PAIRS], BF16, name="sin")
+        nc.sync.dma_start(out=cos[:], in_=freqs_cos.rearrange("(t p) j -> p t j", p=P))
+        nc.sync.dma_start(out=sin[:], in_=freqs_sin.rearrange("(t p) j -> p t j", p=P))
+        gain = {}
+        for which, gain_hbm in (("q", qn_w), ("k", kn_w)):
+            gain[which] = keep.tile([P, HEAD], BF16, name="gain_" + which)
+            nc.sync.dma_start(out=gain[which][:], in_=gain_hbm.partition_broadcast(P))
         bias = {}
 
         def load_bias(c):
-            b_t = keep.tile([P, N_TILE], BF16, name="bias%d" % c)
-            b_src, col0 = col_tiles[c][2], col_tiles[c][3]
-            nc.sync.dma_start(out=b_t[:], in_=b_src[col0 : col0 + N_TILE].partition_broadcast(P))
-            bias[c] = b_t
+            bias[c] = keep.tile([P, COLS], BF16, name="bias%d" % c)
+            bias_hbm, col0 = sources[c][2], sources[c][3]
+            nc.sync.dma_start(out=bias[c][:], in_=bias_hbm[col0 : col0 + COLS].partition_broadcast(P))
 
         load_bias(0)
-        w_codes[1], w_planes[1] = load_col_tile(1, "w1", CHUNK_RUNS, False)
-        for c in range(1, 6):
+        w_codes_of[1], w_plane_of[1] = load_column_tile(1, "w1", SECOND_SWEEP_RUNS, False)
+        for c in range(1, V_TILE + 1):
             load_bias(c)
-        for c in (2, 3, 4):
-            w_codes[c], w_planes[c] = load_col_tile(c, "w%d" % c, ((0, 16),), False)
+        for c in range(2, V_TILE):
+            w_codes_of[c], w_plane_of[c] = load_column_tile(c, "w%d" % c, WHOLE_RUN, False)
 
-        tabs = {}
-        for nm in ("q", "k"):
-            g3 = gains[nm][:].rearrange("p (j e) -> p j e", e=2)
-            gsw = keep.tile([P, HEAD // 2, 2], F32, name="gsw_" + nm)
+        tables = {}
+        for which in ("q", "k"):
+            gain_pairs = gain[which][:].rearrange("p (j e) -> p j e", e=2)
+            swapped_gain = keep.tile([P, PAIRS, 2], F32, name="swapped_gain_" + which)
             nc.vector.tensor_scalar(
-                out=gsw[:, :, 0:1], in0=g3[:, :, 1:2], scalar1=-1.0, scalar2=None, op0=ALU.mult
+                out=swapped_gain[:, :, 0:1], in0=gain_pairs[:, :, 1:2], scalar1=-1.0, scalar2=None, op0=ALU.mult
             )
-            nc.vector.tensor_copy(out=gsw[:, :, 1:2], in_=g3[:, :, 0:1])
-            tab_c = keep.tile([P, POS_TILES, HEAD], F32, name="tabc_" + nm)
-            tab_s = keep.tile([P, POS_TILES, HEAD], F32, name="tabs_" + nm)
-            for t in range(POS_TILES):
+            nc.vector.tensor_copy(out=swapped_gain[:, :, 1:2], in_=gain_pairs[:, :, 0:1])
+            tab_same = keep.tile([P, POSITION_TILES, HEAD], F32, name="tab_same_" + which)
+            tab_swap = keep.tile([P, POSITION_TILES, HEAD], F32, name="tab_swap_" + which)
+            for t in range(POSITION_TILES):
                 nc.vector.tensor_tensor(
-                    out=tab_c[:, t, :].rearrange("p (j e) -> p j e", e=2),
-                    in0=g3,
-                    in1=cos_raw[:, t, :].unsqueeze(2).to_broadcast([P, HEAD // 2, 2]),
+                    out=tab_same[:, t, :].rearrange("p (j e) -> p j e", e=2),
+                    in0=gain_pairs,
+                    in1=cos[:, t, :].unsqueeze(2).to_broadcast([P, PAIRS, 2]),
                     op=ALU.mult,
                 )
                 nc.vector.tensor_tensor(
-                    out=tab_s[:, t, :].rearrange("p (j e) -> p j e", e=2),
-                    in0=gsw[:],
-                    in1=sin_raw[:, t, :].unsqueeze(2).to_broadcast([P, HEAD // 2, 2]),
+                    out=tab_swap[:, t, :].rearrange("p (j e) -> p j e", e=2),
+                    in0=swapped_gain[:],
+                    in1=sin[:, t, :].unsqueeze(2).to_broadcast([P, PAIRS, 2]),
                     op=ALU.mult,
                 )
-            tabs[nm] = (tab_c, tab_s)
+            tables[which] = (tab_same, tab_swap)
 
-        def new_acc(n):
-            acc = psum.tile([P, n], F32, name="acc", tag="acc")
-            return acc
 
-        def mm(acc, c, m, g, n0=0, n=N_TILE):
+        def multiply(bank, c, m, g, col0, ncols):
             nc.tensor.matmul_mx(
-                out=acc[:],
-                lhsT=x_codes[g][:, 256 * m : 256 * (m + 1)].bitcast(FP4X4),
-                lhsT_scale=x_planes[g][:, P * m : P * (m + 1)],
-                rhs=w_codes[c][g][:, 2 * n0 : 2 * (n0 + n)].bitcast(FP4X4),
-                rhs_scale=w_planes[c][g][:, n0 : n0 + n],
+                out=bank[:],
+                lhsT=x_codes_of[g][:, 2 * P * m : 2 * P * (m + 1)].bitcast(FP4X4),
+                lhsT_scale=x_plane_of[g][:, P * m : P * (m + 1)],
+                rhs=w_codes_of[c][g][:, 2 * col0 : 2 * (col0 + ncols)].bitcast(FP4X4),
+                rhs_scale=w_plane_of[c][g][:, col0 : col0 + ncols],
                 start=(g == 0),
                 stop=(g == PASSES - 1),
             )
 
-        def out_slice(c, m, n0=0, n=N_TILE):
-            col0, dst = col_tiles[c][3], col_tiles[c][4]
-            return dst[P * m : P * (m + 1), col0 + n0 : col0 + n0 + n]
+        def output_rows(c, m, col0, ncols):
+            first, out = sources[c][3] + col0, sources[c][4]
+            return out[P * m : P * (m + 1), first : first + ncols]
 
-        def stage_a(acc, c, m, n0=0, n=N_TILE):
-            if c == 5:
-                res = work.tile([P, n], F32, name="res", tag="res", bufs=3)
-                nc.vector.tensor_tensor(out=res[:], in0=acc[:], in1=bias[c][:, n0 : n0 + n], op=ALU.add)
-                nc.sync.dma_start(out=out_slice(c, m, n0, n), in_=res[:])
-                return None
-            h = work.tile([P, N_TILE], F32, name="h", tag="h", bufs=8)
-            nc.vector.tensor_tensor(out=h[:], in0=acc[:], in1=bias[c][:], op=ALU.add)
-            ss = work.tile([P, HEADS_PER_TILE], F32, name="ss", tag="ss", bufs=9)
-            rms = work.tile([P, HEADS_PER_TILE], F32, name="rms", tag="rms", bufs=9)
-            for n in range(HEADS_PER_TILE):
-                junk = work.tile([P, HEAD], F32, name="junk", tag="junk", bufs=2)
+        def finish_v(bank, m, col0, ncols):
+            result = work.tile([P, ncols], F32, name="result", tag="result", bufs=3)
+            nc.vector.tensor_tensor(
+                out=result[:], in0=bank[:], in1=bias[V_TILE][:, col0 : col0 + ncols], op=ALU.add
+            )
+            nc.sync.dma_start(out=output_rows(V_TILE, m, col0, ncols), in_=result[:])
+
+        def empty_bank(bank, c):
+            h = work.tile([P, COLS], F32, name="h", tag="h", bufs=TOKEN_TILES)
+            nc.vector.tensor_tensor(out=h[:], in0=bank[:], in1=bias[c][:], op=ALU.add)
+            sum_sq = work.tile([P, HEADS], F32, name="sum_sq", tag="sum_sq", bufs=TOKEN_TILES + 1)
+            rms = work.tile([P, HEADS], F32, name="rms", tag="rms", bufs=TOKEN_TILES + 1)
+            for n in range(HEADS):
+                squares = work.tile([P, HEAD], F32, name="squares", tag="squares", bufs=2)
                 nc.scalar.activation(
-                    out=junk[:],
+                    out=squares[:],
                     in_=h[:, HEAD * n : HEAD * (n + 1)],
                     func=ACT.Square,
-                    accum_out=ss[:, n : n + 1],
+                    accum_out=sum_sq[:, n : n + 1],
                 )
-            nc.scalar.activation(out=rms[:], in_=ss[:], func=ACT.Sqrt, bias=eps_t[:], scale=1.0 / HEAD)
+            nc.scalar.activation(out=rms[:], in_=sum_sq[:], func=ACT.Sqrt, bias=eps[:], scale=1.0 / HEAD)
             return h, rms
 
-        def stage_b(state, c, m):
-            if state is None:
-                return
-            h, rms = state
-            tab_c, tab_s = tabs["q" if c < 4 else "k"]
-            t = m % POS_TILES
-            t1 = work.tile([P, N_TILE], F32, name="t1", tag="t1", bufs=3)
-            t2 = work.tile([P, N_TILE], F32, name="t2", tag="t2", bufs=2)
+        def rotate_and_store(h, rms, c, m):
+            tab_same, tab_swap = tables["k" if c == K_TILE else "q"]
+            t = m % POSITION_TILES
+            rotated = work.tile([P, COLS], F32, name="rotated", tag="rotated", bufs=3)
+            swap_part = work.tile([P, COLS], F32, name="swap_part", tag="swap_part", bufs=2)
             nc.vector.tensor_tensor(
-                out=t1[:].rearrange("p (n d) -> p n d", d=HEAD),
+                out=rotated[:].rearrange("p (n d) -> p n d", d=HEAD),
                 in0=h[:].rearrange("p (n d) -> p n d", d=HEAD),
-                in1=tab_c[:, t, :].unsqueeze(1).to_broadcast([P, HEADS_PER_TILE, HEAD]),
+                in1=tab_same[:, t, :].unsqueeze(1).to_broadcast([P, HEADS, HEAD]),
                 op=ALU.mult,
             )
             nc.vector.tensor_tensor(
-                out=t2[:].rearrange("p (n j e) -> p n j e", n=HEADS_PER_TILE, e=2),
-                in0=h[:].rearrange("p (n j e) -> p n j e", n=HEADS_PER_TILE, e=2)[:, :, :, ::-1],
-                in1=tab_s[:, t, :]
+                out=swap_part[:].rearrange("p (n j e) -> p n j e", n=HEADS, e=2),
+                in0=h[:].rearrange("p (n j e) -> p n j e", n=HEADS, e=2)[:, :, :, ::-1],
+                in1=tab_swap[:, t, :]
                 .rearrange("p (j e) -> p j e", e=2)
                 .unsqueeze(1)
-                .to_broadcast([P, HEADS_PER_TILE, HEAD // 2, 2]),
+                .to_broadcast([P, HEADS, PAIRS, 2]),
                 op=ALU.mult,
             )
-            nc.vector.tensor_tensor(out=t1[:], in0=t1[:], in1=t2[:], op=ALU.add)
-            rstd = work.tile([P, HEADS_PER_TILE], F32, name="rstd", tag="rstd", bufs=3)
-            nc.vector.reciprocal(out=rstd[:], in_=rms[:])
-            res = work.tile([P, N_TILE], F32, name="res", tag="res", bufs=3)
-            for n in range(HEADS_PER_TILE):
+            nc.vector.tensor_tensor(out=rotated[:], in0=rotated[:], in1=swap_part[:], op=ALU.add)
+            inv_rms = work.tile([P, HEADS], F32, name="inv_rms", tag="inv_rms", bufs=3)
+            nc.vector.reciprocal(out=inv_rms[:], in_=rms[:])
+            result = work.tile([P, COLS], F32, name="result", tag="result", bufs=3)
+            for n in range(HEADS):
                 nc.scalar.activation(
-                    out=res[:, HEAD * n : HEAD * (n + 1)],
-                    in_=t1[:, HEAD * n : HEAD * (n + 1)],
+                    out=result[:, HEAD * n : HEAD * (n + 1)],
+                    in_=rotated[:, HEAD * n : HEAD * (n + 1)],
                     func=ACT.Copy,
-                    scale=rstd[:, n : n + 1],
+                    scale=inv_rms[:, n : n + 1],
                 )
-            nc.scalar.dma_start(out=out_slice(c, m), in_=res[:])
+            nc.scalar.dma_start(out=output_rows(c, m, 0, COLS), in_=result[:])
 
-        def sweep(c, ms):
-            accs = [new_acc(N_TILE) for m in ms]
+        def sweep(c, token_tiles, col0=0, ncols=COLS):
+            banks = [psum.tile([P, ncols], F32, name="bank", tag="bank") for m in token_tiles]
             for g in range(PASSES):
-                for acc, m in zip(accs, ms):
-                    mm(acc, c, m, g)
-            states = [stage_a(acc, c, m) for acc, m in zip(accs, ms)]
-            return states
+                for bank, m in zip(banks, token_tiles):
+                    multiply(bank, c, m, g, col0, ncols)
+            if c == V_TILE:
+                for bank, m in zip(banks, token_tiles):
+                    finish_v(bank, m, col0, ncols)
+            else:
+                emptied = [empty_bank(bank, c) for bank in banks]
+                for (h, rms), m in zip(emptied, token_tiles):
+                    rotate_and_store(h, rms, c, m)
 
-        ms_all = list(range(M_TILES))
-        states = sweep(0, ms_all)
-        for st, m in zip(states, ms_all):
-            stage_b(st, 0, m)
-        for ms in (ms_all[:4], ms_all[4:]):
-            states = sweep(1, ms)
-            for st, m in zip(states, ms):
-                stage_b(st, 1, m)
-        w_codes[5], w_planes[5] = load_col_tile(5, "s", STREAM_RUNS, True)
-        for c in (2, 3, 4, 5):
-            for m in ms_all:
-                if c == 5 and m == M_TILES - 1:
-                    break
-                states = sweep(c, [m])
-                stage_b(states[0], c, m)
-        for n0 in (0, N_TILE // 2):
-            acc = new_acc(N_TILE // 2)
-            for g in range(PASSES):
-                mm(acc, 5, M_TILES - 1, g, n0, N_TILE // 2)
-            stage_a(acc, 5, M_TILES - 1, n0, N_TILE // 2)
+        all_token_tiles = list(range(TOKEN_TILES))
+        sweep(0, all_token_tiles)
+        sweep(1, all_token_tiles[:4])
+        sweep(1, all_token_tiles[4:])
+        w_codes_of[V_TILE], w_plane_of[V_TILE] = load_column_tile(V_TILE, "w0", FIRST_SWEEP_RUNS, True)
+        single_tiles = [(c, m) for c in range(2, V_TILE + 1) for m in all_token_tiles]
+        for c, m in single_tiles[:-1]:
+            sweep(c, [m])
+        c, m = single_tiles[-1]
+        for col0 in (0, COLS // 2):
+            sweep(c, [m], col0, COLS // 2)

@@ -26,7 +26,6 @@ V_TILE = 5
 EPS = 1e-5
 FLOPS = 2 * TOKENS * (PASSES * K_PASS) * ((V_TILE + 1) * COLS)
 
-FIRST_SWEEP_RUNS = ((0, 1), (1, 4), (4, 8), (8, 12), (12, 16))
 SECOND_SWEEP_RUNS = ((0, 4), (4, 8), (8, 12), (12, 16))
 WHOLE_RUN = ((0, PASSES),)
 
@@ -125,24 +124,22 @@ def tile_llamacausalselfattention_pa_kernel(
         w_plane_of = {0: {}}
 
         x_run_planes = keep.tile([P, 1, TOKENS], U8, name="xp0", tag="xp0", align_bytes=64)
-        w_run_planes = keep.tile([P, 1, COLS], U8, name="w0p0", tag="w0p0", align_bytes=64)
         fill_quadrant(x_run_planes, x_scales, 0, TOKENS)
         fill_quadrant(x_run_planes, x_scales, 1, TOKENS)
         x_codes_of[0] = load_codes("xc0", x_words, 0, 1, 0, 2 * TOKENS)[:, 0, :]
         w_codes_of[0][0] = load_codes("w0c0", Wq_words, 0, 1, 0, 2 * COLS)[:, 0, :]
         fill_quadrant(x_run_planes, x_scales, 2, TOKENS)
         fill_quadrant(x_run_planes, x_scales, 3, TOKENS)
-        for quad in range(QUADRANTS):
-            fill_quadrant(w_run_planes, Wq_scales, quad, COLS)
         x_plane_of[0] = x_run_planes[:, 0, :]
-        w_plane_of[0][0] = w_run_planes[:, 0, :]
 
-        for g0, g1 in FIRST_SWEEP_RUNS[1:]:
-            x_run_planes = load_planes("xp%d" % g0, x_scales, g0, g1, 0, TOKENS)
+        for g0, g1 in SECOND_SWEEP_RUNS:
             w_run_planes = load_planes("w0p%d" % g0, Wq_scales, g0, g1, 0, COLS)
+            first = max(g0, 1)
+            x_run_planes = load_planes("xp%d" % first, x_scales, first, g1, 0, TOKENS)
             for g in range(g0, g1):
-                x_plane_of[g] = x_run_planes[:, g - g0, :]
                 w_plane_of[0][g] = w_run_planes[:, g - g0, :]
+            for g in range(first, g1):
+                x_plane_of[g] = x_run_planes[:, g - first, :]
                 x_codes_of[g] = load_codes("xc%d" % g, x_words, g, g + 1, 0, 2 * TOKENS)[:, 0, :]
                 w_codes_of[0][g] = load_codes("w0c%d" % g, Wq_words, g, g + 1, 0, 2 * COLS)[:, 0, :]
 
@@ -287,7 +284,7 @@ def tile_llamacausalselfattention_pa_kernel(
         sweep(0, all_token_tiles)
         sweep(1, all_token_tiles[:4])
         sweep(1, all_token_tiles[4:])
-        w_codes_of[V_TILE], w_plane_of[V_TILE] = load_column_tile(V_TILE, "w0", FIRST_SWEEP_RUNS, True)
+        w_codes_of[V_TILE], w_plane_of[V_TILE] = load_column_tile(V_TILE, "w0", SECOND_SWEEP_RUNS, True)
         single_tiles = [(c, m) for c in range(2, V_TILE + 1) for m in all_token_tiles]
         for c, m in single_tiles[:-1]:
             sweep(c, [m])

@@ -29,7 +29,7 @@ FLOPS = 2 * TOKENS * (PASSES * K_PASS) * ((V_TILE + 1) * COLS)
 SECOND_SWEEP_RUNS = ((0, 4), (4, 8), (8, 12), (12, 16))
 WHOLE_RUN = ((0, PASSES),)
 
-WARM_MATMULS = 9
+WARM_MATMULS = 6
 
 
 def tile_llamacausalselfattention_pa_kernel(

@@ -285,9 +285,11 @@ def tile_llamacausalselfattention_pa_kernel(
         sweep(1, all_token_tiles[:4])
         sweep(1, all_token_tiles[4:])
         w_codes_of[V_TILE], w_plane_of[V_TILE] = load_column_tile(V_TILE, "w0", SECOND_SWEEP_RUNS, True)
-        single_tiles = [(c, m) for c in range(2, V_TILE + 1) for m in all_token_tiles]
-        for c, m in single_tiles[:-1]:
-            sweep(c, [m])
-        c, m = single_tiles[-1]
+        for c in range(2, V_TILE):
+            sweep(c, all_token_tiles[:4])
+            sweep(c, all_token_tiles[4:])
+        sweep(V_TILE, all_token_tiles[:4])
+        for m in all_token_tiles[4:-1]:
+            sweep(V_TILE, [m])
         for col0 in (0, COLS // 2):
-            sweep(c, [m], col0, COLS // 2)
+            sweep(V_TILE, [all_token_tiles[-1]], col0, COLS // 2)

@@ -128,12 +128,14 @@ def tile_llamacausalselfattention_pa_kernel(
         fill_quadrant(x_run_planes, x_scales, 1, TOKENS)
         x_codes_of[0] = load_codes("xc0", x_words, 0, 1, 0, 2 * TOKENS)[:, 0, :]
         w_codes_of[0][0] = load_codes("w0c0", Wq_words, 0, 1, 0, 2 * COLS)[:, 0, :]
-        fill_quadrant(x_run_planes, x_scales, 2, TOKENS)
-        fill_quadrant(x_run_planes, x_scales, 3, TOKENS)
-        x_plane_of[0] = x_run_planes[:, 0, :]
+        x_first_plane = x_run_planes
+        x_plane_of[0] = x_first_plane[:, 0, :]
 
         for g0, g1 in SECOND_SWEEP_RUNS:
             w_run_planes = load_planes("w0p%d" % g0, Wq_scales, g0, g1, 0, COLS)
+            if g0 == 0:
+                fill_quadrant(x_first_plane, x_scales, 2, TOKENS)
+                fill_quadrant(x_first_plane, x_scales, 3, TOKENS)
             first = max(g0, 1)
             x_run_planes = load_planes("xp%d" % first, x_scales, first, g1, 0, TOKENS)
             for g in range(g0, g1):

@@ -74,76 +74,62 @@ def tile_llamacausalselfattention_pa_kernel(
             nc.tensor.matmul(out=dummy_bank[:], lhsT=zeros[:, 0:P], rhs=zeros[:], start=True, stop=True)
 
 
-        def load_codes(tag, words, g0, g1, byte0, nbytes):
-            codes = keep.tile([P, g1 - g0, nbytes], U8, name=tag, tag=tag, align_bytes=64)
+        def operand_tiles(tag, ncols):
+            codes = keep.tile([P, PASSES, 2 * ncols], U8, name=tag + "c", tag=tag + "c", align_bytes=64)
+            planes = keep.tile([P, PASSES, ncols], U8, name=tag + "p", tag=tag + "p", align_bytes=64)
+            return codes, planes
+
+        def load_codes(codes, words, g0, g1, byte0):
+            nbytes = codes.shape[2]
             nc.sync.dma_start(
-                out=codes[:].bitcast(I32),
+                out=codes[:, g0:g1, :].bitcast(I32),
                 in_=words[g0:g1, :, byte0 : byte0 + nbytes].rearrange("g p b -> p g b").bitcast(I32),
             )
-            return codes
 
-        def load_planes(tag, scales, g0, g1, col0, ncols):
-            planes = keep.tile([P, g1 - g0, ncols], U8, name=tag, tag=tag, align_bytes=64)
-            nc.vector.memset(planes[:].bitcast(I32), 0)
+        def load_planes(planes, scales, g0, g1, col0):
+            ncols = planes.shape[2]
+            nc.vector.memset(planes[:, g0:g1, :].bitcast(I32), 0)
             for quad in range(QUADRANTS):
                 nc.sync.dma_start(
-                    out=planes[32 * quad : 32 * quad + 4, :, :].bitcast(I32),
+                    out=planes[32 * quad : 32 * quad + 4, g0:g1, :].bitcast(I32),
                     in_=scales[g0:g1, 4 * quad : 4 * quad + 4, col0 : col0 + ncols]
                     .rearrange("g r n -> r g n")
                     .bitcast(I32),
                 )
-            return planes
 
-        def fill_quadrant(planes, scales, quad, ncols):
+        def fill_quadrant(planes, scales, quad):
+            ncols = planes.shape[2]
             nc.sync.dma_start(
                 out=planes[32 * quad : 32 * quad + 32, 0, :].bitcast(I32),
                 in_=scales.rearrange("g r n -> (g r) n")[4 * quad : 4 * quad + 32, 0:ncols].bitcast(I32),
             )
 
-        def load_column_tile(c, tag, plane_runs, codes_by_pass):
+        def load_column_tile(c, tag, runs):
             words, scales, col0 = sources[c][0], sources[c][1], sources[c][3]
-            codes_of = {}
-            plane_of = {}
-            for g0, g1 in plane_runs:
-                planes = load_planes("%sp%d" % (tag, g0), scales, g0, g1, col0, COLS)
-                for g in range(g0, g1):
-                    plane_of[g] = planes[:, g - g0, :]
-                if codes_by_pass:
-                    for g in range(g0, g1):
-                        codes = load_codes("%sc%d" % (tag, g), words, g, g + 1, 2 * col0, 2 * COLS)
-                        codes_of[g] = codes[:, 0, :]
-                else:
-                    codes = load_codes("%sc%d" % (tag, g0), words, g0, g1, 2 * col0, 2 * COLS)
-                    for g in range(g0, g1):
-                        codes_of[g] = codes[:, g - g0, :]
-            return codes_of, plane_of
+            w_codes[c], w_planes[c] = operand_tiles(tag, COLS)
+            for g0, g1 in runs:
+                load_planes(w_planes[c], scales, g0, g1, col0)
+                load_codes(w_codes[c], words, g0, g1, 2 * col0)
 
-        x_codes_of = {}
-        x_plane_of = {}
-        w_codes_of = {0: {}}
-        w_plane_of = {0: {}}
+        w_codes = {}
+        w_planes = {}
+        x_codes, x_planes = operand_tiles("x", TOKENS)
+        w_codes[0], w_planes[0] = operand_tiles("w0", COLS)
 
-        x_run_planes = keep.tile([P, 1, TOKENS], U8, name="xp0", tag="xp0", align_bytes=64)
-        fill_quadrant(x_run_planes, x_scales, 0, TOKENS)
-        fill_quadrant(x_run_planes, x_scales, 1, TOKENS)
-        x_codes_of[0] = load_codes("xc0", x_words, 0, 1, 0, 2 * TOKENS)[:, 0, :]
-        w_codes_of[0][0] = load_codes("w0c0", Wq_words, 0, 1, 0, 2 * COLS)[:, 0, :]
-        x_first_plane = x_run_planes
-        x_plane_of[0] = x_first_plane[:, 0, :]
-
+        fill_quadrant(x_planes, x_scales, 0)
+        fill_quadrant(x_planes, x_scales, 1)
+        load_codes(x_codes, x_words, 0, 1, 0)
+        load_codes(w_codes[0], Wq_words, 0, 1, 0)
         for g0, g1 in SECOND_SWEEP_RUNS:
-            w_run_planes = load_planes("w0p%d" % g0, Wq_scales, g0, g1, 0, COLS)
+            load_planes(w_planes[0], Wq_scales, g0, g1, 0)
             if g0 == 0:
-                fill_quadrant(x_first_plane, x_scales, 2, TOKENS)
-                fill_quadrant(x_first_plane, x_scales, 3, TOKENS)
+                fill_quadrant(x_planes, x_scales, 2)
+                fill_quadrant(x_planes, x_scales, 3)
             first = max(g0, 1)
-            x_run_planes = load_planes("xp%d" % first, x_scales, first, g1, 0, TOKENS)
-            for g in range(g0, g1):
-                w_plane_of[0][g] = w_run_planes[:, g - g0, :]
+            load_planes(x_planes, x_scales, first, g1, 0)
             for g in range(first, g1):
-                x_plane_of[g] = x_run_planes[:, g - first, :]
-                x_codes_of[g] = load_codes("xc%d" % g, x_words, g, g + 1, 0, 2 * TOKENS)[:, 0, :]
-                w_codes_of[0][g] = load_codes("w0c%d" % g, Wq_words, g, g + 1, 0, 2 * COLS)[:, 0, :]
+                load_codes(x_codes, x_words, g, g + 1, 0)
+                load_codes(w_codes[0], Wq_words, g, g + 1, 0)
 
         eps = keep.tile([P, 1], F32, name="eps")
         nc.vector.memset(eps[:], EPS)
@@ -166,11 +152,11 @@ def tile_llamacausalselfattention_pa_kernel(
             nc.sync.dma_start(out=bias[c][:], in_=bias_hbm[col0 : col0 + COLS].partition_broadcast(P))
 
         load_bias(0)
-        w_codes_of[1], w_plane_of[1] = load_column_tile(1, "w1", SECOND_SWEEP_RUNS, False)
+        load_column_tile(1, "w1", SECOND_SWEEP_RUNS)
         for c in range(1, V_TILE + 1):
             load_bias(c)
         for c in range(2, V_TILE):
-            w_codes_of[c], w_plane_of[c] = load_column_tile(c, "w%d" % c, WHOLE_RUN, False)
+            load_column_tile(c, "w%d" % c, WHOLE_RUN)
 
         tables = {}
         for which in ("q", "k"):
@@ -201,10 +187,10 @@ def tile_llamacausalselfattention_pa_kernel(
         def multiply(bank, c, m, g, col0, ncols):
             nc.tensor.matmul_mx(
                 out=bank[:],
-                lhsT=x_codes_of[g][:, 2 * P * m : 2 * P * (m + 1)].bitcast(FP4X4),
-                lhsT_scale=x_plane_of[g][:, P * m : P * (m + 1)],
-                rhs=w_codes_of[c][g][:, 2 * col0 : 2 * (col0 + ncols)].bitcast(FP4X4),
-                rhs_scale=w_plane_of[c][g][:, col0 : col0 + ncols],
+                lhsT=x_codes[:, g, 2 * P * m : 2 * P * (m + 1)].bitcast(FP4X4),
+                lhsT_scale=x_planes[:, g, P * m : P * (m + 1)],
+                rhs=w_codes[c][:, g, 2 * col0 : 2 * (col0 + ncols)].bitcast(FP4X4),
+                rhs_scale=w_planes[c][:, g, col0 : col0 + ncols],
                 start=(g == 0),
                 stop=(g == PASSES - 1),
             )
@@ -286,7 +272,7 @@ def tile_llamacausalselfattention_pa_kernel(
         sweep(0, all_token_tiles)
         sweep(1, all_token_tiles[:4])
         sweep(1, all_token_tiles[4:])
-        w_codes_of[V_TILE], w_plane_of[V_TILE] = load_column_tile(V_TILE, "w0", SECOND_SWEEP_RUNS, True)
+        load_column_tile(V_TILE, "w0", WHOLE_RUN)
         for c in range(2, V_TILE):
             sweep(c, all_token_tiles[:4])
             sweep(c, all_token_tiles[4:])

@@ -199,12 +199,13 @@ def tile_llamacausalselfattention_pa_kernel(
             first, out = sources[c][3] + col0, sources[c][4]
             return out[P * m : P * (m + 1), first : first + ncols]
 
-        def finish_v(bank, m, col0, ncols):
+        def finish_v(bank, m, col0, ncols, queue=None):
             result = work.tile([P, ncols], F32, name="result", tag="result", bufs=3)
             nc.vector.tensor_tensor(
                 out=result[:], in0=bank[:], in1=bias[V_TILE][:, col0 : col0 + ncols], op=ALU.add
             )
-            nc.sync.dma_start(out=output_rows(V_TILE, m, col0, ncols), in_=result[:])
+            issuer = nc.sync if queue is None else queue
+            issuer.dma_start(out=output_rows(V_TILE, m, col0, ncols), in_=result[:])
 
         def empty_bank(bank, c):
             h = work.tile([P, COLS], F32, name="h", tag="h", bufs=TOKEN_TILES)
@@ -262,7 +263,7 @@ def tile_llamacausalselfattention_pa_kernel(
                     multiply(bank, c, m, g, col0, ncols)
             if c == V_TILE:
                 for bank, m in zip(banks, token_tiles):
-                    finish_v(bank, m, col0, ncols)
+                    finish_v(bank, m, col0, ncols, nc.scalar if (ncols < COLS and col0 == 0) else None)
             else:
                 emptied = [empty_bank(bank, c) for bank in banks]
                 for (h, rms), m in zip(emptied, token_tiles):

@@ -117,13 +117,13 @@ def tile_llamacausalselfattention_pa_kernel(
         w_codes[0], w_planes[0] = operand_tiles("w0", COLS)
 
         fill_quadrant(x_planes, x_scales, 0)
-        fill_quadrant(x_planes, x_scales, 1)
+        fill_quadrant(x_planes, x_scales, 2)
         load_codes(x_codes, x_words, 0, 1, 0)
         load_codes(w_codes[0], Wq_words, 0, 1, 0)
         for g0, g1 in SECOND_SWEEP_RUNS:
             load_planes(w_planes[0], Wq_scales, g0, g1, 0)
             if g0 == 0:
-                fill_quadrant(x_planes, x_scales, 2)
+                fill_quadrant(x_planes, x_scales, 1)
                 fill_quadrant(x_planes, x_scales, 3)
             first = max(g0, 1)
             load_planes(x_planes, x_scales, first, g1, 0)

@@ -89,7 +89,7 @@ def tile_llamacausalselfattention_pa_kernel(
         def load_planes(planes, scales, g0, g1, col0):
             ncols = planes.shape[2]
             nc.vector.memset(planes[:, g0:g1, :].bitcast(I32), 0)
-            for quad in range(QUADRANTS):
+            for quad in (0, 2, 1, 3):
                 nc.sync.dma_start(
                     out=planes[32 * quad : 32 * quad + 4, g0:g1, :].bitcast(I32),
                     in_=scales[g0:g1, 4 * quad : 4 * quad + 4, col0 : col0 + ncols]

@@ -123,8 +123,13 @@ def tile_llamacausalselfattention_pa_kernel(
         for g0, g1 in SECOND_SWEEP_RUNS:
             load_planes(w_planes[0], Wq_scales, g0, g1, 0)
             if g0 == 0:
-                fill_quadrant(x_planes, x_scales, 1)
-                fill_quadrant(x_planes, x_scales, 3)
+                for quad in (1, 3):
+                    nc.vector.memset(x_planes[32 * quad : 32 * quad + 32, 0, :].bitcast(I32), 0)
+                for quad in (1, 3):
+                    nc.sync.dma_start(
+                        out=x_planes[32 * quad : 32 * quad + 4, 0, :].bitcast(I32),
+                        in_=x_scales[0, 4 * quad : 4 * quad + 4, :].bitcast(I32),
+                    )
             first = max(g0, 1)
             load_planes(x_planes, x_scales, first, g1, 0)
             for g in range(first, g1):

@@ -21,7 +21,7 @@ HEAD = 128
 HEADS = COLS // HEAD
 PAIRS = HEAD // 2
 QUADRANTS = 4
-K_TILE = 4
+K_TILE = 0
 V_TILE = 5
 EPS = 1e-5
 FLOPS = 2 * TOKENS * (PASSES * K_PASS) * ((V_TILE + 1) * COLS)
@@ -57,8 +57,8 @@ def tile_llamacausalselfattention_pa_kernel(
     q_out = out_0.rearrange("b t h d -> (b t) (h d)")
     k_out = out_1.rearrange("b t h d -> (b t) (h d)")
     v_out = out_2.rearrange("b t h d -> (b t) (h d)")
-    sources = [(Wq_words, Wq_scales, bq, COLS * c, q_out) for c in range(K_TILE)]
-    sources.append((Wk_words, Wk_scales, bk, 0, k_out))
+    sources = [(Wk_words, Wk_scales, bk, 0, k_out)]
+    sources.extend([(Wq_words, Wq_scales, bq, COLS * c, q_out) for c in range(V_TILE - 1)])
     sources.append((Wv_words, Wv_scales, bv, 0, v_out))
 
     with ExitStack() as ctx:
@@ -119,9 +119,9 @@ def tile_llamacausalselfattention_pa_kernel(
         fill_quadrant(x_planes, x_scales, 0)
         fill_quadrant(x_planes, x_scales, 2)
         load_codes(x_codes, x_words, 0, 1, 0)
-        load_codes(w_codes[0], Wq_words, 0, 1, 0)
+        load_codes(w_codes[0], Wk_words, 0, 1, 0)
         for g0, g1 in SECOND_SWEEP_RUNS:
-            load_planes(w_planes[0], Wq_scales, g0, g1, 0)
+            load_planes(w_planes[0], Wk_scales, g0, g1, 0)
             if g0 == 0:
                 for quad in (1, 3):
                     nc.vector.memset(x_planes[32 * quad : 32 * quad + 32, 0, :].bitcast(I32), 0)
@@ -134,7 +134,7 @@ def tile_llamacausalselfattention_pa_kernel(
             load_planes(x_planes, x_scales, first, g1, 0)
             for g in range(first, g1):
                 load_codes(x_codes, x_words, g, g + 1, 0)
-                load_codes(w_codes[0], Wq_words, g, g + 1, 0)
+                load_codes(w_codes[0], Wk_words, g, g + 1, 0)
 
         eps = keep.tile([P, 1], F32, name="eps")
         nc.vector.memset(eps[:], EPS)

@@ -274,6 +274,15 @@ def tile_llamacausalselfattention_pa_kernel(
                 for (h, rms), m in zip(emptied, token_tiles):
                     rotate_and_store(h, rms, c, m)
 
+        nc.tensor.matmul_mx(
+            out=dummy_bank[:],
+            lhsT=w_codes[0][:, 0, 0 : 2 * P].bitcast(FP4X4),
+            lhsT_scale=w_planes[0][:, 0, 0:P],
+            rhs=w_codes[0][:, 0, :].bitcast(FP4X4),
+            rhs_scale=w_planes[0][:, 0, :],
+            start=True,
+            stop=True,
+        )
         all_token_tiles = list(range(TOKEN_TILES))
         sweep(0, all_token_tiles)
         sweep(1, all_token_tiles[:4])

@@ -31,6 +31,8 @@ WHOLE_RUN = ((0, PASSES),)
 
 WARM_MATMULS = 6
 
+SPLIT = 8
+
 
 def tile_llamacausalselfattention_pa_kernel(
     tc,
@@ -189,15 +191,15 @@ def tile_llamacausalselfattention_pa_kernel(
             tables[which] = (tab_same, tab_swap)
 
 
-        def multiply(bank, c, m, g, col0, ncols):
+        def multiply(bank, c, m, g, col0, ncols, first=0, last=PASSES - 1):
             nc.tensor.matmul_mx(
                 out=bank[:],
                 lhsT=x_codes[:, g, 2 * P * m : 2 * P * (m + 1)].bitcast(FP4X4),
                 lhsT_scale=x_planes[:, g, P * m : P * (m + 1)],
                 rhs=w_codes[c][:, g, 2 * col0 : 2 * (col0 + ncols)].bitcast(FP4X4),
                 rhs_scale=w_planes[c][:, g, col0 : col0 + ncols],
-                start=(g == 0),
-                stop=(g == PASSES - 1),
+                start=(g == first),
+                stop=(g == last),
             )
 
         def output_rows(c, m, col0, ncols):
@@ -294,5 +296,22 @@ def tile_llamacausalselfattention_pa_kernel(
         sweep(V_TILE, all_token_tiles[:4])
         for m in all_token_tiles[4:-1]:
             sweep(V_TILE, [m])
-        for col0 in (0, COLS // 2):
-            sweep(V_TILE, [all_token_tiles[-1]], col0, COLS // 2)
+        last_m = all_token_tiles[-1]
+        half = COLS // 2
+        quarter = COLS // 4
+        sweep(V_TILE, [last_m], 0, half)
+        early_bank = psum.tile([P, half], F32, name="bank", tag="bank")
+        for g in range(SPLIT):
+            multiply(early_bank, V_TILE, last_m, g, half, half, 0, SPLIT - 1)
+        early = work.tile([P, half], F32, name="early", tag="early", bufs=1)
+        nc.vector.tensor_tensor(out=early[:], in0=early_bank[:], in1=bias[V_TILE][:, half:COLS], op=ALU.add)
+        for piece in range(2):
+            late_bank = psum.tile([P, quarter], F32, name="bank", tag="bank")
+            col0 = half + quarter * piece
+            for g in range(SPLIT, PASSES):
+                multiply(late_bank, V_TILE, last_m, g, col0, quarter, SPLIT, PASSES - 1)
+            result = work.tile([P, quarter], F32, name="result", tag="result", bufs=3)
+            nc.vector.tensor_tensor(
+                out=result[:], in0=late_bank[:], in1=early[:, quarter * piece : quarter * (piece + 1)], op=ALU.add
+            )
+            (nc.scalar if piece == 0 else nc.sync).dma_start(out=output_rows(V_TILE, last_m, col0, quarter), in_=result[:])

@@ -29,7 +29,7 @@ FLOPS = 2 * TOKENS * (PASSES * K_PASS) * ((V_TILE + 1) * COLS)
 SECOND_SWEEP_RUNS = ((0, 4), (4, 8), (8, 12), (12, 16))
 WHOLE_RUN = ((0, PASSES),)
 
-WARM_MATMULS = 6
+WARM_MATMULS = 7
 
 SPLIT = 8
 
@@ -69,11 +69,17 @@ def tile_llamacausalselfattention_pa_kernel(
         work = ctx.enter_context(tc.tile_pool(name="work", bufs=2))
         psum = ctx.enter_context(tc.psum_pool(name="psum", bufs=8))
 
-        zeros = keep.tile([P, COLS], BF16, name="zeros")
+        zeros = keep.tile([P, 2], BF16, name="zeros")
         nc.gpsimd.memset(zeros[:], 0.0)
         dummy_bank = psum.tile([P, COLS], F32, name="bank", tag="bank")
         for i in range(WARM_MATMULS):
-            nc.tensor.matmul(out=dummy_bank[:], lhsT=zeros[:, 0:P], rhs=zeros[:], start=True, stop=True)
+            nc.tensor.matmul(
+                out=dummy_bank[:],
+                lhsT=zeros[:, 0:1].to_broadcast([P, P]),
+                rhs=zeros[:, 0:1].to_broadcast([P, COLS]),
+                start=True,
+                stop=True,
+            )
 
 
         def operand_tiles(tag, ncols):

@@ -31,7 +31,7 @@ WHOLE_RUN = ((0, PASSES),)
 
 WARM_MATMULS = 7
 
-SPLIT = 8
+SPLIT = 10
 
 
 def tile_llamacausalselfattention_pa_kernel(
@@ -303,21 +303,17 @@ def tile_llamacausalselfattention_pa_kernel(
         for m in all_token_tiles[4:-1]:
             sweep(V_TILE, [m])
         last_m = all_token_tiles[-1]
-        half = COLS // 2
-        quarter = COLS // 4
-        sweep(V_TILE, [last_m], 0, half)
-        early_bank = psum.tile([P, half], F32, name="bank", tag="bank")
+        early_bank = psum.tile([P, COLS], F32, name="bank", tag="bank")
         for g in range(SPLIT):
-            multiply(early_bank, V_TILE, last_m, g, half, half, 0, SPLIT - 1)
-        early = work.tile([P, half], F32, name="early", tag="early", bufs=1)
-        nc.vector.tensor_tensor(out=early[:], in0=early_bank[:], in1=bias[V_TILE][:, half:COLS], op=ALU.add)
-        for piece in range(2):
-            late_bank = psum.tile([P, quarter], F32, name="bank", tag="bank")
-            col0 = half + quarter * piece
+            multiply(early_bank, V_TILE, last_m, g, 0, COLS, 0, SPLIT - 1)
+        early = work.tile([P, COLS], F32, name="early", tag="early", bufs=1)
+        nc.vector.tensor_tensor(out=early[:], in0=early_bank[:], in1=bias[V_TILE][:], op=ALU.add)
+        for col0, ncols in ((0, COLS // 2), (COLS // 2, COLS // 4), (3 * COLS // 4, COLS // 4)):
+            late_bank = psum.tile([P, ncols], F32, name="bank", tag="bank")
             for g in range(SPLIT, PASSES):
-                multiply(late_bank, V_TILE, last_m, g, col0, quarter, SPLIT, PASSES - 1)
-            result = work.tile([P, quarter], F32, name="result", tag="result", bufs=3)
-            nc.vector.tensor_tensor(
-                out=result[:], in0=late_bank[:], in1=early[:, quarter * piece : quarter * (piece + 1)], op=ALU.add
+                multiply(late_bank, V_TILE, last_m, g, col0, ncols, SPLIT, PASSES - 1)
+            result = work.tile([P, ncols], F32, name="result", tag="result", bufs=3)
+            nc.vector.tensor_tensor(out=result[:], in0=late_bank[:], in1=early[:, col0 : col0 + ncols], op=ALU.add)
+            (nc.sync if col0 + ncols == COLS else nc.scalar).dma_start(
+                out=output_rows(V_TILE, last_m, col0, ncols), in_=result[:]
             )
-            (nc.scalar if piece == 0 else nc.sync).dma_start(out=output_rows(V_TILE, last_m, col0, quarter), in_=result[:])

@@ -293,13 +293,14 @@ def tile_llamacausalselfattention_pa_kernel(
         )
         all_token_tiles = list(range(TOKEN_TILES))
         sweep(0, all_token_tiles)
-        sweep(1, all_token_tiles[:4])
-        sweep(1, all_token_tiles[4:])
+        sweep(1, all_token_tiles[:2])
+        sweep(1, all_token_tiles[2:])
         load_column_tile(V_TILE, "w0", WHOLE_RUN)
         for c in range(2, V_TILE):
-            sweep(c, all_token_tiles[:4])
-            sweep(c, all_token_tiles[4:])
-        sweep(V_TILE, all_token_tiles[:4])
+            sweep(c, all_token_tiles[:2])
+            sweep(c, all_token_tiles[2:])
+        sweep(V_TILE, all_token_tiles[:2])
+        sweep(V_TILE, all_token_tiles[2:4])
         for m in all_token_tiles[4:-1]:
             sweep(V_TILE, [m])
         last_m = all_token_tiles[-1]

@@ -31,7 +31,7 @@ WHOLE_RUN = ((0, PASSES),)
 
 WARM_MATMULS = 7
 
-SPLIT = 10
+SPLIT = 8
 
 
 def tile_llamacausalselfattention_pa_kernel(

from contextlib import ExitStack

import concourse.mybir as mybir

F32 = mybir.dt.float32
BF16 = mybir.dt.bfloat16
I32 = mybir.dt.int32
U8 = mybir.dt.uint8
FP4X4 = mybir.dt.float4_e2m1fn_x4
ALU = mybir.AluOpType
ACT = mybir.ActivationFunctionType

P = 128
K_PASS = 512
PASSES = 16
TOKENS = 1024
TOKEN_TILES = TOKENS // P
POSITION_TILES = 4
COLS = 512
HEAD = 128
HEADS = COLS // HEAD
PAIRS = HEAD // 2
QUADRANTS = 4
K_TILE = 0
V_TILE = 5
EPS = 1e-5
FLOPS = 2 * TOKENS * (PASSES * K_PASS) * ((V_TILE + 1) * COLS)

SECOND_SWEEP_RUNS = ((0, 4), (4, 8), (8, 12), (12, 16))
WHOLE_RUN = ((0, PASSES),)

WARM_MATMULS = 7

SPLIT = 8


def tile_llamacausalselfattention_pa_kernel(
    tc,
    x_words,
    x_scales,
    Wq_words,
    Wq_scales,
    bq,
    Wk_words,
    Wk_scales,
    bk,
    Wv_words,
    Wv_scales,
    bv,
    qn_w,
    kn_w,
    freqs_cos,
    freqs_sin,
    out_0,
    out_1,
    out_2,
):
    nc = tc.nc
    q_out = out_0.rearrange("b t h d -> (b t) (h d)")
    k_out = out_1.rearrange("b t h d -> (b t) (h d)")
    v_out = out_2.rearrange("b t h d -> (b t) (h d)")
    sources = [(Wk_words, Wk_scales, bk, 0, k_out)]
    sources.extend([(Wq_words, Wq_scales, bq, COLS * c, q_out) for c in range(V_TILE - 1)])
    sources.append((Wv_words, Wv_scales, bv, 0, v_out))

    with ExitStack() as ctx:
        ctx.enter_context(tc.manual_schedule())
        keep = ctx.enter_context(tc.tile_pool(name="keep", bufs=1))
        work = ctx.enter_context(tc.tile_pool(name="work", bufs=2))
        psum = ctx.enter_context(tc.psum_pool(name="psum", bufs=8))

        zeros = keep.tile([P, 2], BF16, name="zeros")
        nc.gpsimd.memset(zeros[:], 0.0)
        dummy_bank = psum.tile([P, COLS], F32, name="bank", tag="bank")
        for i in range(WARM_MATMULS):
            nc.tensor.matmul(
                out=dummy_bank[:],
                lhsT=zeros[:, 0:1].to_broadcast([P, P]),
                rhs=zeros[:, 0:1].to_broadcast([P, COLS]),
                start=True,
                stop=True,
            )


        def operand_tiles(tag, ncols):
            codes = keep.tile([P, PASSES, 2 * ncols], U8, name=tag + "c", tag=tag + "c", align_bytes=64)
            planes = keep.tile([P, PASSES, ncols], U8, name=tag + "p", tag=tag + "p", align_bytes=64)
            return codes, planes

        def load_codes(codes, words, g0, g1, byte0):
            nbytes = codes.shape[2]
            nc.sync.dma_start(
                out=codes[:, g0:g1, :].bitcast(I32),
                in_=words[g0:g1, :, byte0 : byte0 + nbytes].rearrange("g p b -> p g b").bitcast(I32),
            )

        def load_planes(planes, scales, g0, g1, col0):
            ncols = planes.shape[2]
            nc.vector.memset(planes[:, g0:g1, :].bitcast(I32), 0)
            for quad in (0, 2, 1, 3):
                nc.sync.dma_start(
                    out=planes[32 * quad : 32 * quad + 4, g0:g1, :].bitcast(I32),
                    in_=scales[g0:g1, 4 * quad : 4 * quad + 4, col0 : col0 + ncols]
                    .rearrange("g r n -> r g n")
                    .bitcast(I32),
                )

        def fill_quadrant(planes, scales, quad):
            ncols = planes.shape[2]
            nc.sync.dma_start(
                out=planes[32 * quad : 32 * quad + 32, 0, :].bitcast(I32),
                in_=scales.rearrange("g r n -> (g r) n")[4 * quad : 4 * quad + 32, 0:ncols].bitcast(I32),
            )

        def load_column_tile(c, tag, runs):
            words, scales, col0 = sources[c][0], sources[c][1], sources[c][3]
            w_codes[c], w_planes[c] = operand_tiles(tag, COLS)
            for g0, g1 in runs:
                load_planes(w_planes[c], scales, g0, g1, col0)
                load_codes(w_codes[c], words, g0, g1, 2 * col0)

        w_codes = {}
        w_planes = {}
        x_codes, x_planes = operand_tiles("x", TOKENS)
        w_codes[0], w_planes[0] = operand_tiles("w0", COLS)

        fill_quadrant(x_planes, x_scales, 0)
        fill_quadrant(x_planes, x_scales, 2)
        load_codes(x_codes, x_words, 0, 1, 0)
        load_codes(w_codes[0], Wk_words, 0, 1, 0)
        for g0, g1 in SECOND_SWEEP_RUNS:
            load_planes(w_planes[0], Wk_scales, g0, g1, 0)
            if g0 == 0:
                for quad in (1, 3):
                    nc.vector.memset(x_planes[32 * quad : 32 * quad + 32, 0, :].bitcast(I32), 0)
                for quad in (1, 3):
                    nc.sync.dma_start(
                        out=x_planes[32 * quad : 32 * quad + 4, 0, :].bitcast(I32),
                        in_=x_scales[0, 4 * quad : 4 * quad + 4, :].bitcast(I32),
                    )
            first = max(g0, 1)
            load_planes(x_planes, x_scales, first, g1, 0)
            for g in range(first, g1):
                load_codes(x_codes, x_words, g, g + 1, 0)
                load_codes(w_codes[0], Wk_words, g, g + 1, 0)

        eps = keep.tile([P, 1], F32, name="eps")
        nc.vector.memset(eps[:], EPS)
        table_warmer = keep.tile([P, 1], F32, name="table_warmer")
        nc.scalar.activation(out=table_warmer[:], in_=eps[:], func=ACT.Sqrt)

        cos = keep.tile([P, POSITION_TILES, PAIRS], BF16, name="cos")
        sin = keep.tile([P, POSITION_TILES, PAIRS], BF16, name="sin")
        nc.sync.dma_start(out=cos[:], in_=freqs_cos.rearrange("(t p) j -> p t j", p=P))
        nc.sync.dma_start(out=sin[:], in_=freqs_sin.rearrange("(t p) j -> p t j", p=P))
        gain = {}
        for which, gain_hbm in (("q", qn_w), ("k", kn_w)):
            gain[which] = keep.tile([P, HEAD], BF16, name="gain_" + which)
            nc.sync.dma_start(out=gain[which][:], in_=gain_hbm.partition_broadcast(P))
        bias = {}

        def load_bias(c):
            bias[c] = keep.tile([P, COLS], BF16, name="bias%d" % c)
            bias_hbm, col0 = sources[c][2], sources[c][3]
            nc.sync.dma_start(out=bias[c][:], in_=bias_hbm[col0 : col0 + COLS].partition_broadcast(P))

        load_bias(0)
        load_column_tile(1, "w1", SECOND_SWEEP_RUNS)
        for c in range(1, V_TILE + 1):
            load_bias(c)
        for c in range(2, V_TILE):
            load_column_tile(c, "w%d" % c, WHOLE_RUN)

        tables = {}
        for which in ("q", "k"):
            gain_pairs = gain[which][:].rearrange("p (j e) -> p j e", e=2)
            swapped_gain = keep.tile([P, PAIRS, 2], F32, name="swapped_gain_" + which)
            nc.vector.tensor_scalar(
                out=swapped_gain[:, :, 0:1], in0=gain_pairs[:, :, 1:2], scalar1=-1.0, scalar2=None, op0=ALU.mult
            )
            nc.vector.tensor_copy(out=swapped_gain[:, :, 1:2], in_=gain_pairs[:, :, 0:1])
            tab_same = keep.tile([P, POSITION_TILES, HEAD], F32, name="tab_same_" + which)
            tab_swap = keep.tile([P, POSITION_TILES, HEAD], F32, name="tab_swap_" + which)
            for t in range(POSITION_TILES):
                nc.vector.tensor_tensor(
                    out=tab_same[:, t, :].rearrange("p (j e) -> p j e", e=2),
                    in0=gain_pairs,
                    in1=cos[:, t, :].unsqueeze(2).to_broadcast([P, PAIRS, 2]),
                    op=ALU.mult,
                )
                nc.vector.tensor_tensor(
                    out=tab_swap[:, t, :].rearrange("p (j e) -> p j e", e=2),
                    in0=swapped_gain[:],
                    in1=sin[:, t, :].unsqueeze(2).to_broadcast([P, PAIRS, 2]),
                    op=ALU.mult,
                )
            tables[which] = (tab_same, tab_swap)


        def multiply(bank, c, m, g, col0, ncols, first=0, last=PASSES - 1):
            nc.tensor.matmul_mx(
                out=bank[:],
                lhsT=x_codes[:, g, 2 * P * m : 2 * P * (m + 1)].bitcast(FP4X4),
                lhsT_scale=x_planes[:, g, P * m : P * (m + 1)],
                rhs=w_codes[c][:, g, 2 * col0 : 2 * (col0 + ncols)].bitcast(FP4X4),
                rhs_scale=w_planes[c][:, g, col0 : col0 + ncols],
                start=(g == first),
                stop=(g == last),
            )

        def output_rows(c, m, col0, ncols):
            first, out = sources[c][3] + col0, sources[c][4]
            return out[P * m : P * (m + 1), first : first + ncols]

        def finish_v(bank, m, col0, ncols, queue=None):
            result = work.tile([P, ncols], F32, name="result", tag="result", bufs=3)
            nc.vector.tensor_tensor(
                out=result[:], in0=bank[:], in1=bias[V_TILE][:, col0 : col0 + ncols], op=ALU.add
            )
            issuer = nc.sync if queue is None else queue
            issuer.dma_start(out=output_rows(V_TILE, m, col0, ncols), in_=result[:])

        def empty_bank(bank, c):
            h = work.tile([P, COLS], F32, name="h", tag="h", bufs=TOKEN_TILES)
            nc.vector.tensor_tensor(out=h[:], in0=bank[:], in1=bias[c][:], op=ALU.add)
            sum_sq = work.tile([P, HEADS], F32, name="sum_sq", tag="sum_sq", bufs=TOKEN_TILES + 1)
            rms = work.tile([P, HEADS], F32, name="rms", tag="rms", bufs=TOKEN_TILES + 1)
            for n in range(HEADS):
                squares = work.tile([P, HEAD], F32, name="squares", tag="squares", bufs=2)
                nc.scalar.activation(
                    out=squares[:],
                    in_=h[:, HEAD * n : HEAD * (n + 1)],
                    func=ACT.Square,
                    accum_out=sum_sq[:, n : n + 1],
                )
            nc.scalar.activation(out=rms[:], in_=sum_sq[:], func=ACT.Sqrt, bias=eps[:], scale=1.0 / HEAD)
            return h, rms

        def rotate_and_store(h, rms, c, m):
            tab_same, tab_swap = tables["k" if c == K_TILE else "q"]
            t = m % POSITION_TILES
            rotated = work.tile([P, COLS], F32, name="rotated", tag="rotated", bufs=3)
            swap_part = work.tile([P, COLS], F32, name="swap_part", tag="swap_part", bufs=2)
            nc.vector.tensor_tensor(
                out=rotated[:].rearrange("p (n d) -> p n d", d=HEAD),
                in0=h[:].rearrange("p (n d) -> p n d", d=HEAD),
                in1=tab_same[:, t, :].unsqueeze(1).to_broadcast([P, HEADS, HEAD]),
                op=ALU.mult,
            )
            nc.vector.tensor_tensor(
                out=swap_part[:].rearrange("p (n j e) -> p n j e", n=HEADS, e=2),
                in0=h[:].rearrange("p (n j e) -> p n j e", n=HEADS, e=2)[:, :, :, ::-1],
                in1=tab_swap[:, t, :]
                .rearrange("p (j e) -> p j e", e=2)
                .unsqueeze(1)
                .to_broadcast([P, HEADS, PAIRS, 2]),
                op=ALU.mult,
            )
            nc.vector.tensor_tensor(out=rotated[:], in0=rotated[:], in1=swap_part[:], op=ALU.add)
            inv_rms = work.tile([P, HEADS], F32, name="inv_rms", tag="inv_rms", bufs=3)
            nc.vector.reciprocal(out=inv_rms[:], in_=rms[:])
            result = work.tile([P, COLS], F32, name="result", tag="result", bufs=3)
            for n in range(HEADS):
                nc.scalar.activation(
                    out=result[:, HEAD * n : HEAD * (n + 1)],
                    in_=rotated[:, HEAD * n : HEAD * (n + 1)],
                    func=ACT.Copy,
                    scale=inv_rms[:, n : n + 1],
                )
            nc.scalar.dma_start(out=output_rows(c, m, 0, COLS), in_=result[:])

        def sweep(c, token_tiles, col0=0, ncols=COLS):
            banks = [psum.tile([P, ncols], F32, name="bank", tag="bank") for m in token_tiles]
            for g in range(PASSES):
                for bank, m in zip(banks, token_tiles):
                    multiply(bank, c, m, g, col0, ncols)
            if c == V_TILE:
                for bank, m in zip(banks, token_tiles):
                    finish_v(bank, m, col0, ncols, nc.scalar if (ncols < COLS and col0 == 0) else None)
            else:
                emptied = [empty_bank(bank, c) for bank in banks]
                for (h, rms), m in zip(emptied, token_tiles):
                    rotate_and_store(h, rms, c, m)

        nc.tensor.matmul_mx(
            out=dummy_bank[:],
            lhsT=w_codes[0][:, 0, 0 : 2 * P].bitcast(FP4X4),
            lhsT_scale=w_planes[0][:, 0, 0:P],
            rhs=w_codes[0][:, 0, :].bitcast(FP4X4),
            rhs_scale=w_planes[0][:, 0, :],
            start=True,
            stop=True,
        )
        all_token_tiles = list(range(TOKEN_TILES))
        sweep(0, all_token_tiles)
        sweep(1, all_token_tiles[:2])
        sweep(1, all_token_tiles[2:])
        load_column_tile(V_TILE, "w0", WHOLE_RUN)
        for c in range(2, V_TILE):
            sweep(c, all_token_tiles[:2])
            sweep(c, all_token_tiles[2:])
        sweep(V_TILE, all_token_tiles[:2])
        sweep(V_TILE, all_token_tiles[2:4])
        for m in all_token_tiles[4:-1]:
            sweep(V_TILE, [m])
        last_m = all_token_tiles[-1]
        early_bank = psum.tile([P, COLS], F32, name="bank", tag="bank")
        for g in range(SPLIT):
            multiply(early_bank, V_TILE, last_m, g, 0, COLS, 0, SPLIT - 1)
        early = work.tile([P, COLS], F32, name="early", tag="early", bufs=1)
        nc.vector.tensor_tensor(out=early[:], in0=early_bank[:], in1=bias[V_TILE][:], op=ALU.add)
        for col0, ncols in ((0, COLS // 2), (COLS // 2, COLS // 4), (3 * COLS // 4, COLS // 4)):
            late_bank = psum.tile([P, ncols], F32, name="bank", tag="bank")
            for g in range(SPLIT, PASSES):
                multiply(late_bank, V_TILE, last_m, g, col0, ncols, SPLIT, PASSES - 1)
            result = work.tile([P, ncols], F32, name="result", tag="result", bufs=3)
            nc.vector.tensor_tensor(out=result[:], in0=late_bank[:], in1=early[:, col0 : col0 + ncols], op=ALU.add)
            (nc.sync if col0 + ncols == COLS else nc.scalar).dma_start(
                out=output_rows(V_TILE, last_m, col0, ncols), in_=result[:]
            )
